import numpy as np
import ml_dtypes


def mxq(x, axis, fmt="e4m3"):
    dtype, down = {"e4m3": (ml_dtypes.float8_e4m3fn, 7), "e5m2": (ml_dtypes.float8_e5m2, 14)}[fmt]
    v = np.moveaxis(np.asarray(x, np.float32).astype(ml_dtypes.bfloat16).astype(np.float64), axis, -1)
    blocks = v.reshape(v.shape[:-1] + (-1, 32))
    amax = np.abs(blocks).max(-1, keepdims=True)
    byte = np.maximum(np.where(amax > 0, np.frexp(amax)[1] - 1 + 127, 0) - down, 1)
    scale = np.exp2(byte - 127.0)
    codes = (blocks / scale).astype(np.float32).astype(dtype).astype(np.float64)
    return np.moveaxis((codes * scale).reshape(v.shape), -1, axis)


WIDE = False


def mx_kscale(k):
    if not WIDE:
        return np.ones(k)
    levels = np.array([10, -10, 5, -5, 0])
    a = np.random.permutation(np.resize(levels, k // 512 * 4)).reshape(k // 512, 4)
    idx = np.arange(k)
    return np.exp2(a[idx // 512, idx % 128 // 32])


BF16 = ml_dtypes.bfloat16


def bf(x):
    return np.asarray(x, np.float32).astype(BF16)


def f64(x):
    return np.asarray(x).astype(np.float64)


B, DH, DO, L = 4096, 256, 512, 128


def setup_inputs():
    s = mx_kscale(2 * DH)
    t = mx_kscale(DO)
    return {"sbj_vec": bf(np.random.standard_normal((B, DH)) * s[:DH]),
            "obj_vec": bf(np.random.standard_normal((B, DH)) * s[DH:]),
            "W1": bf(np.random.standard_normal((2 * DH, DO)) * 1.28 / np.sqrt(2 * DH) / s[:, None] * t),
            "b1": bf(np.random.standard_normal(DO) * 0.1 * t),
            "W2": bf(np.random.standard_normal((DO, DO)) * 12.0 / DO / t[:, None]),
            "b2": bf(np.random.standard_normal(DO) * 0.1),
            "label_vecs": bf(np.random.standard_normal((L, DO)) * 8.0 / np.sqrt(DO))}


def reference(sbj_vec, obj_vec, W1, b1, W2, b2, label_vecs):
    x = np.concatenate([f64(sbj_vec), f64(obj_vec)], axis=1)
    hidden = (mxq(np.maximum(x, 0.0), 1, "e4m3") @ mxq(f64(W1), 0, "e4m3")) + f64(b1)
    emb = (mxq(np.maximum(hidden, 0.0), 1, "e4m3") @ mxq(f64(W2), 0, "e4m3")) + f64(b2)
    lab = f64(label_vecs)
    scores = np.empty((emb.shape[0], lab.shape[0]))
    for l in range(lab.shape[0]):
        diff = np.maximum(lab[l][None, :] - emb, 0.0)
        scores[:, l] = -np.sqrt(np.sum(diff * diff, axis=1))
    return scores

@@ -1,0 +1,328 @@
+from contextlib import ExitStack
+
+import concourse.mybir as mybir
+from concourse.masks import make_identity
+
+F32 = mybir.dt.float32
+BF16 = mybir.dt.bfloat16
+U32 = mybir.dt.uint32
+U8 = mybir.dt.uint8
+FP8X4 = mybir.dt.float8_e4m3fn_x4
+ALU = mybir.AluOpType
+ACT = mybir.ActivationFunctionType
+
+P = 128
+B, DH, DO, L = 4096, 256, 512, 128
+NJ = B // P
+NC = DO // P
+GROUP = 4
+NCOL = GROUP * P
+
+NA = 4
+NV = 4
+NT = NJ - NA
+AHEAD = 2
+MBUFS = 3
+PIN = False
+RB = 7
+LBN = 4
+
+FLOPS = 2 * B * (2 * DH) * DO + 2 * B * DO * DO + 4 * B * L * DO
+
+
+def split_ranges():
+    n_r = -(-NT // RB)
+    res = []
+    j0 = 0
+    v_done = 0
+    for r in range(n_r):
+        nb = NT // n_r + (1 if r < NT % n_r else 0)
+        v_upto = (NV * (r + 1)) // n_r
+        nv = v_upto - v_done
+        v_done = v_upto
+        owners = [((bi + 1) * nv) // nb > (bi * nv) // nb for bi in range(nb)]
+        res.append((j0, nb, owners))
+        j0 += nb
+    return res
+
+
+def tile_relationembedding_t_kernel(tc, sbj_vec, obj_vec, W1, b1, W2, b2, label_vecs, out):
+    nc = tc.nc
+    ranges = split_ranges()
+    wmax = max(nb for (j0, nb, owners) in ranges) * P
+    with ExitStack() as ctx:
+        ctx.enter_context(nc.allow_non_contiguous_dma(reason="rows of 512 bytes and more"))
+        keep = ctx.enter_context(tc.tile_pool(name="keep", bufs=1))
+        ident_f = keep.tile([P, P], F32, name="ident_f")
+        make_identity(nc, ident_f[:])
+        lab_t = keep.tile([P, NC, L], F32, name="lab_t")
+        bias_t = keep.tile([P, 8], F32, name="bias_t")
+        emb_t = keep.tile([P, NC, NT * P], F32, name="emb_t")
+        emb_a = keep.tile([P, max(NA, 1), DO], F32, name="emb_a")
+        sums = keep.tile([P, NJ, L], F32, name="sums")
+
+        with tc.tile_pool(name="prep", bufs=1) as prep, tc.tile_pool(name="work", bufs=2) as work, tc.psum_pool(
+            name="ps1", bufs=2
+        ) as ps1:
+            one = prep.tile([P, 1], F32, name="one")
+            nc.vector.memset(one[:], 1.0)
+            nc.scalar.activation(out=one[:], in_=one[:], func=ACT.Sqrt)
+
+            ident_b = prep.tile([P, P], BF16, name="ident_b")
+            make_identity(nc, ident_b[:])
+            rows = prep.tile([P, P], BF16, name="rows")
+            nc.vector.memset(rows[:], 0.0)
+
+            x_all = prep.tile([P, NJ, 2 * DH], BF16, name="x_all")
+            sbj_v = sbj_vec.rearrange("(p j) k -> p j k", j=NJ)
+            obj_v = obj_vec.rearrange("(p j) k -> p j k", j=NJ)
+
+            def load_x(j0, j1):
+                nc.sync.dma_start(out=x_all[:, j0:j1, 0:DH], in_=sbj_v[:, j0:j1, :])
+                nc.sync.dma_start(out=x_all[:, j0:j1, DH : 2 * DH], in_=obj_v[:, j0:j1, :])
+
+            w1_raw = prep.tile([P, 4, DO], BF16, name="w1_raw")
+            nc.sync.dma_start(
+                out=w1_raw[:].rearrange("p (u e) h -> p u (e h)", u=2),
+                in_=W1.rearrange("(u p e) h -> p u (e h)", u=2, e=2),
+            )
+            load_x(0, 8)
+            nc.sync.dma_start(out=rows[0:4, :], in_=b1.rearrange("(t p) -> t p", p=P))
+            nc.sync.dma_start(out=rows[4:8, :], in_=b2.rearrange("(t p) -> t p", p=P))
+            w2_raw = prep.tile([P, 4, DO], BF16, name="w2_raw")
+            nc.sync.dma_start(out=w2_raw[:], in_=W2.rearrange("(t p) d -> p t d", p=P))
+            lab_sb = prep.tile([P, DO], BF16, name="lab_sb")
+            nc.sync.dma_start(out=lab_sb[:], in_=label_vecs)
+            b2_bc = prep.tile([P, DO], BF16, name="b2_bc")
+            if NA > 0:
+                nc.sync.dma_start(out=b2_bc[:], in_=b2.partition_broadcast(P))
+            load_x(8, 16)
+            load_x(16, 24)
+            load_x(24, 32)
+
+            def quantise(src, codes, scales, nm):
+                grouped = work.tile([P, NCOL, 4], BF16, name=nm, tag="grouped", align_bytes=64)
+                nc.vector.tensor_copy(out=grouped[:], in_=src.rearrange("p t w -> p w t"))
+                nc.vector.quantize_mx(
+                    out=codes.bitcast(FP8X4), scales=scales, in_=grouped[:].rearrange("p w t -> p (w t)")
+                )
+
+            w1_q = prep.tile([P, DO], U32, name="w1_q", align_bytes=64)
+            w1_s = prep.tile([P, DO], U8, name="w1_s", align_bytes=64)
+            quantise(w1_raw[:], w1_q[:], w1_s[:], "w1_g")
+            w2_q = prep.tile([P, DO], U32, name="w2_q", align_bytes=64)
+            w2_s = prep.tile([P, DO], U8, name="w2_s", align_bytes=64)
+            quantise(w2_raw[:], w2_q[:], w2_s[:], "w2_g")
+
+            rows_t = ps1.tile([P, P], BF16, name="rows_t", tag="xt")
+            nc.tensor.transpose(rows_t[:], rows[:], ident_b[:])
+            nc.vector.tensor_copy(out=bias_t[:], in_=rows_t[:, 0:8])
+            lab_ps = ps1.tile([P, NC, L], BF16, name="lab_ps", tag="xt")
+            for c in range(NC):
+                nc.tensor.transpose(lab_ps[:, c, :], lab_sb[:, c * P : (c + 1) * P], ident_b[:])
+            nc.vector.tensor_copy(out=lab_t[:], in_=lab_ps[:])
+
+            for g in range(NJ // GROUP):
+                xr = work.tile([P, GROUP, 2 * DH], BF16, name="xr")
+                nc.vector.tensor_scalar_max(out=xr[:], in0=x_all[:, g * GROUP : (g + 1) * GROUP, :], scalar1=0.0)
+                xg = work.tile([P, NCOL, 4], BF16, name="xg", align_bytes=64)
+                xg_w = xg[:].rearrange("p n t -> p (n t)").bitcast(F32).rearrange("p (n u) -> p n u", u=2)
+                for half in range(2):
+                    xt = ps1.tile([P, 2, 2 * P], F32, name="xt", tag="xt")
+                    for jj in range(2):
+                        for u in range(2):
+                            nc.tensor.transpose(
+                                xt[:, u, jj * P : (jj + 1) * P],
+                                xr[:, 2 * half + jj, u * DH : (u + 1) * DH].bitcast(F32),
+                                ident_f[:],
+                            )
+                    nc.scalar.copy(
+                        out=xg_w[:, half * 2 * P : (half + 1) * 2 * P, :], in_=xt[:].rearrange("p u n -> p n u")
+                    )
+                x_q = work.tile([P, NCOL], U32, name="x_q", align_bytes=64)
+                x_s = work.tile([P, NCOL], U8, name="x_s", align_bytes=64)
+                nc.vector.quantize_mx(
+                    out=x_q[:].bitcast(FP8X4), scales=x_s[:], in_=xg[:].rearrange("p n t -> p (n t)")
+                )
+                hb = work.tile([P, 4, NCOL], BF16, name="hb")
+                for t in range(4):
+                    hp = ps1.tile([P, NCOL], F32, name="hp")
+                    nc.tensor.matmul_mx(
+                        out=hp[:],
+                        lhsT=w1_q[:, t * P : (t + 1) * P].bitcast(FP8X4),
+                        lhsT_scale=w1_s[:, t * P : (t + 1) * P],
+                        rhs=x_q[:].bitcast(FP8X4),
+                        rhs_scale=x_s[:],
+                        start=True,
+                        stop=True,
+                    )
+                    nc.scalar.activation(out=hb[:, t, :], in_=hp[:], func=ACT.Relu, bias=bias_t[:, t : t + 1], scale=1.0)
+                h_q = work.tile([P, NCOL], U32, name="h_q", align_bytes=64)
+                h_s = work.tile([P, NCOL], U8, name="h_s", align_bytes=64)
+                quantise(hb[:], h_q[:], h_s[:], "hg")
+                nt = max(0, min(GROUP, NT - g * GROUP))
+                if nt > 0:
+                    for c in range(NC):
+                        ep = ps1.tile([P, NCOL], F32, name="ep")
+                        nc.tensor.matmul_mx(
+                            out=ep[:],
+                            lhsT=w2_q[:, c * P : (c + 1) * P].bitcast(FP8X4),
+                            lhsT_scale=w2_s[:, c * P : (c + 1) * P],
+                            rhs=h_q[:].bitcast(FP8X4),
+                            rhs_scale=h_s[:],
+                            start=True,
+                            stop=True,
+                        )
+                        nc.vector.tensor_scalar_add(
+                            out=emb_t[:, c, g * NCOL : g * NCOL + nt * P],
+                            in0=ep[:, 0 : nt * P],
+                            scalar1=bias_t[:, 4 + c : 5 + c],
+                        )
+                for jj in range(nt, GROUP):
+                    ea = ps1.tile([P, DO], F32, name="ea", tag="ep")
+                    nc.tensor.matmul_mx(
+                        out=ea[:],
+                        lhsT=h_q[:, jj * P : (jj + 1) * P].bitcast(FP8X4),
+                        lhsT_scale=h_s[:, jj * P : (jj + 1) * P],
+                        rhs=w2_q[:].bitcast(FP8X4),
+                        rhs_scale=w2_s[:],
+                        start=True,
+                        stop=True,
+                    )
+                    nc.vector.tensor_tensor(out=emb_a[:, g * GROUP + jj - NT, :], in0=ea[:], in1=b2_bc[:], op=ALU.add)
+
+        out_v = out.rearrange("(p j) l -> p j l", j=NJ)
+        with ExitStack() as main:
+            mp = main.enter_context(tc.tile_pool(name="mp", bufs=MBUFS))
+            ap2 = main.enter_context(tc.tile_pool(name="ap2", bufs=2))
+            junk = main.enter_context(tc.tile_pool(name="junk", bufs=4))
+            fin = main.enter_context(tc.tile_pool(name="fin", bufs=2))
+            stp = main.enter_context(tc.tile_pool(name="stp", bufs=1))
+            banks = main.enter_context(tc.psum_pool(name="banks", bufs=8))
+            if PIN:
+                main.enter_context(tc.manual_schedule())
+
+            stats = {}
+            for (j0, nb, owners) in ranges:
+                for bi in range(nb):
+                    if owners[bi]:
+                        stats[j0 + bi] = stp.tile([P, L, 6], F32, name="st%d" % (j0 + bi))
+
+            steps = [(r, l) for r in range(len(ranges)) for l in range(L)]
+            m_tiles = {}
+
+            def pass1(s):
+                r, l = steps[s]
+                j0, nb, owners = ranges[r]
+                m = mp.tile([P, NC, wmax], F32, name="m")
+                m_tiles[s] = m
+                for c in range(NC):
+                    nc.vector.tensor_scalar(
+                        out=m[:, c, 0 : nb * P],
+                        in0=emb_t[:, c, j0 * P : (j0 + nb) * P],
+                        scalar1=lab_t[:, c, l : l + 1],
+                        scalar2=0.0,
+                        op0=ALU.subtract,
+                        op1=ALU.min,
+                    )
+
+            def units(s):
+                r, l = steps[s]
+                j0, nb, owners = ranges[r]
+                m = m_tiles[s]
+                for bi in range(nb):
+                    bank = banks.tile([P, DO], F32, name="bank")
+                    for c in range(NC):
+                        nc.tensor.transpose(bank[:, c * P : (c + 1) * P], m[:, c, bi * P : (bi + 1) * P], ident_f[:])
+                    if owners[bi]:
+                        nc.vector.bn_stats(out=stats[j0 + bi][:, l, :], in_=bank[:])
+                    else:
+                        js = junk.tile([P, DO], F32, name="js")
+                        nc.scalar.activation(
+                            out=js[:], in_=bank[:], func=ACT.Square, accum_out=sums[:, j0 + bi, l : l + 1]
+                        )
+
+            def finish(j0, j1):
+                nb = j1 - j0
+                root = fin.tile([P, RB, L], F32, name="root")
+                nc.scalar.activation(out=root[:, 0:nb, :], in_=sums[:, j0:j1, :], func=ACT.Sqrt)
+                neg = fin.tile([P, RB, L], F32, name="neg")
+                nc.vector.tensor_scalar_mul(out=neg[:, 0:nb, :], in0=root[:, 0:nb, :], scalar1=-1.0)
+                nc.sync.dma_start(out=out_v[:, j0:j1, :], in_=neg[:, 0:nb, :])
+
+            def from_stats(j):
+                sv = stats[j][:].rearrange("p l (h k) -> p l h k", k=3)
+                sq = fin.tile([P, L, 2], F32, name="sq")
+                nc.vector.tensor_tensor(out=sq[:], in0=sv[:, :, :, 1], in1=sv[:, :, :, 1], op=ALU.mult)
+                tot = fin.tile([P, L, 2], F32, name="tot")
+                nc.vector.scalar_tensor_tensor(
+                    out=tot[:], in0=sq[:], scalar=float(DO // 2), in1=sv[:, :, :, 2], op0=ALU.mult, op1=ALU.add
+                )
+                nc.vector.tensor_tensor(out=sums[:, j, :], in0=tot[:, :, 0], in1=tot[:, :, 1], op=ALU.add)
+
+            lb_tiles = {}
+            xs_tiles = {}
+
+            def a_load(l):
+                lb = ap2.tile([P, LBN, DO], BF16, name="lb")
+                lb_tiles[l // LBN] = lb
+                nc.sync.dma_start(
+                    out=lb[:].rearrange("p a d -> p (a d)"),
+                    in_=label_vecs[l : l + LBN, :].rearrange("a d -> (a d)").partition_broadcast(P),
+                )
+
+            def a_diff(l):
+                xs = ap2.tile([P, NA, DO], F32, name="xs")
+                xs_tiles[l] = xs
+                nc.vector.tensor_tensor(
+                    out=xs[:],
+                    in0=emb_a[:],
+                    in1=lb_tiles[l // LBN][:, l % LBN, :].unsqueeze(1).to_broadcast([P, NA, DO]),
+                    op=ALU.subtract,
+                )
+
+            def a_sum(l, ja):
+                jv = junk.tile([P, DO], F32, name="jv")
+                nc.vector.scalar_tensor_tensor(
+                    out=jv[:],
+                    in0=xs_tiles[l][:, ja, :],
+                    scalar=0.0,
+                    in1=xs_tiles[l][:, ja, :],
+                    op0=ALU.min,
+                    op1=ALU.mult,
+                    accum_out=sums[:, NT + ja, l : l + 1],
+                )
+
+            pieces = []
+            if NA > 0:
+                pieces.append((a_load, (0,)))
+                pieces.append((a_diff, (0,)))
+                for l in range(L):
+                    if l % LBN == 0 and l + LBN < L:
+                        pieces.append((a_load, (l + LBN,)))
+                    if l + 1 < L:
+                        pieces.append((a_diff, (l + 1,)))
+                    for ja in range(NA):
+                        pieces.append((a_sum, (l, ja)))
+
+            done = 0
+            for s in range(min(AHEAD, len(steps))):
+                pass1(s)
+            for s in range(len(steps)):
+                if s + AHEAD < len(steps):
+                    pass1(s + AHEAD)
+                units(s)
+                upto = (len(pieces) * (s + 1)) // len(steps)
+                while done < upto:
+                    fn, args = pieces[done]
+                    fn(*args)
+                    done += 1
+                r, l = steps[s]
+                if l == L - 1:
+                    j0, nb, owners = ranges[r]
+                    for bi in range(nb):
+                        if owners[bi]:
+                            from_stats(j0 + bi)
+                    finish(j0, j0 + nb)
+            if NA > 0:
+                finish(NT, NJ)

@@ -23,9 +23,14 @@ NV = 4
 NT = NJ - NA
 AHEAD = 2
 MBUFS = 3
-PIN = False
+PIN = True
 RB = 7
 LBN = 4
+HBK = 3
+BURST_EVERY = 126
+BURST_N = 5
+WARM_N = 8
+NBANK = 7
 
 FLOPS = 2 * B * (2 * DH) * DO + 2 * B * DO * DO + 4 * B * L * DO
 
@@ -60,6 +65,8 @@ def tile_relationembedding_t_kernel(tc, sbj_vec, obj_vec, W1, b1, W2, b2, label_
         emb_t = keep.tile([P, NC, NT * P], F32, name="emb_t")
         emb_a = keep.tile([P, max(NA, 1), DO], F32, name="emb_a")
         sums = keep.tile([P, NJ, L], F32, name="sums")
+        w2_q = keep.tile([P, DO], U32, name="w2_q", align_bytes=64)
+        w2_s = keep.tile([P, DO], U8, name="w2_s", align_bytes=64)
 
         with tc.tile_pool(name="prep", bufs=1) as prep, tc.tile_pool(name="work", bufs=2) as work, tc.psum_pool(
             name="ps1", bufs=2
@@ -110,8 +117,6 @@ def tile_relationembedding_t_kernel(tc, sbj_vec, obj_vec, W1, b1, W2, b2, label_
             w1_q = prep.tile([P, DO], U32, name="w1_q", align_bytes=64)
             w1_s = prep.tile([P, DO], U8, name="w1_s", align_bytes=64)
             quantise(w1_raw[:], w1_q[:], w1_s[:], "w1_g")
-            w2_q = prep.tile([P, DO], U32, name="w2_q", align_bytes=64)
-            w2_s = prep.tile([P, DO], U8, name="w2_s", align_bytes=64)
             quantise(w2_raw[:], w2_q[:], w2_s[:], "w2_g")
 
             rows_t = ps1.tile([P, P], BF16, name="rows_t", tag="xt")
@@ -198,7 +203,8 @@ def tile_relationembedding_t_kernel(tc, sbj_vec, obj_vec, W1, b1, W2, b2, label_
             junk = main.enter_context(tc.tile_pool(name="junk", bufs=4))
             fin = main.enter_context(tc.tile_pool(name="fin", bufs=2))
             stp = main.enter_context(tc.tile_pool(name="stp", bufs=1))
-            banks = main.enter_context(tc.psum_pool(name="banks", bufs=8))
+            banks = main.enter_context(tc.psum_pool(name="banks", bufs=NBANK))
+            beat = main.enter_context(tc.psum_pool(name="beat", bufs=1))
             if PIN:
                 main.enter_context(tc.manual_schedule())
 
@@ -226,11 +232,32 @@ def tile_relationembedding_t_kernel(tc, sbj_vec, obj_vec, W1, b1, W2, b2, label_
                         op1=ALU.min,
                     )
 
+            beat_ps = beat.tile([P, DO], F32, name="beat_ps") if HBK > 0 else None
+            n_units = [0]
+
+            def heartbeat(n):
+                for i in range(n):
+                    nc.tensor.matmul_mx(
+                        out=beat_ps[:],
+                        lhsT=w2_q[:, 0:P].bitcast(FP8X4),
+                        lhsT_scale=w2_s[:, 0:P],
+                        rhs=w2_q[:].bitcast(FP8X4),
+                        rhs_scale=w2_s[:],
+                        start=True,
+                        stop=True,
+                    )
+
             def units(s):
                 r, l = steps[s]
                 j0, nb, owners = ranges[r]
                 m = m_tiles[s]
                 for bi in range(nb):
+                    if HBK > 0:
+                        if BURST_EVERY > 0 and n_units[0] % BURST_EVERY == 0:
+                            heartbeat(WARM_N if n_units[0] == 0 else BURST_N)
+                        elif n_units[0] % HBK == 0:
+                            heartbeat(1)
+                        n_units[0] += 1
                     bank = banks.tile([P, DO], F32, name="bank")
                     for c in range(NC):
                         nc.tensor.transpose(bank[:, c * P : (c + 1) * P], m[:, c, bi * P : (bi + 1) * P], ident_f[:])
@@ -242,12 +269,18 @@ def tile_relationembedding_t_kernel(tc, sbj_vec, obj_vec, W1, b1, W2, b2, label_
                             out=js[:], in_=bank[:], func=ACT.Square, accum_out=sums[:, j0 + bi, l : l + 1]
                         )
 
-            def finish(j0, j1):
+            roots = {}
+
+            def finish_root(j0, j1):
                 nb = j1 - j0
                 root = fin.tile([P, RB, L], F32, name="root")
+                roots[j0] = root
                 nc.scalar.activation(out=root[:, 0:nb, :], in_=sums[:, j0:j1, :], func=ACT.Sqrt)
+
+            def finish_store(j0, j1):
+                nb = j1 - j0
                 neg = fin.tile([P, RB, L], F32, name="neg")
-                nc.vector.tensor_scalar_mul(out=neg[:, 0:nb, :], in0=root[:, 0:nb, :], scalar1=-1.0)
+                nc.vector.tensor_scalar_mul(out=neg[:, 0:nb, :], in0=roots[j0][:, 0:nb, :], scalar1=-1.0)
                 nc.sync.dma_start(out=out_v[:, j0:j1, :], in_=neg[:, 0:nb, :])
 
             def from_stats(j):
@@ -306,6 +339,7 @@ def tile_relationembedding_t_kernel(tc, sbj_vec, obj_vec, W1, b1, W2, b2, label_
                         pieces.append((a_sum, (l, ja)))
 
             done = 0
+            later = {}
             for s in range(min(AHEAD, len(steps))):
                 pass1(s)
             for s in range(len(steps)):
@@ -320,9 +354,14 @@ def tile_relationembedding_t_kernel(tc, sbj_vec, obj_vec, W1, b1, W2, b2, label_
                 r, l = steps[s]
                 if l == L - 1:
                     j0, nb, owners = ranges[r]
-                    for bi in range(nb):
-                        if owners[bi]:
-                            from_stats(j0 + bi)
-                    finish(j0, j0 + nb)
-            if NA > 0:
-                finish(NT, NJ)
+                    later[s + 1] = [(from_stats, (j0 + bi,)) for bi in range(nb) if owners[bi]]
+                    later[s + 3] = [(finish_root, (j0, j0 + nb))]
+                    later[s + 5] = [(finish_store, (j0, j0 + nb))]
+                for fn, args in later.get(s, []):
+                    fn(*args)
+            for s in range(len(steps), len(steps) + 6):
+                for fn, args in later.get(s, []):
+                    fn(*args)
+                if s == len(steps) and NA > 0:
+                    finish_root(NT, NJ)
+                    finish_store(NT, NJ)

@@ -18,16 +18,17 @@ NC = DO // P
 GROUP = 4
 NCOL = GROUP * P
 
-NA = 4
-NV = 4
+NA = 2
+NV = 6
 NT = NJ - NA
 AHEAD = 2
 MBUFS = 3
 PIN = True
-RB = 7
+RB = 10
 LBN = 4
-HBK = 3
-BURST_EVERY = 126
+PARTS = 2
+HBK = 4
+BURST_EVERY = 128
 BURST_N = 5
 WARM_N = 8
 NBANK = 7
@@ -178,11 +179,20 @@ def tile_relationembedding_t_kernel(tc, sbj_vec, obj_vec, W1, b1, W2, b2, label_
                             start=True,
                             stop=True,
                         )
-                        nc.vector.tensor_scalar_add(
-                            out=emb_t[:, c, g * NCOL : g * NCOL + nt * P],
-                            in0=ep[:, 0 : nt * P],
-                            scalar1=bias_t[:, 4 + c : 5 + c],
-                        )
+                        if c % 2 == 0:
+                            nc.vector.tensor_scalar_add(
+                                out=emb_t[:, c, g * NCOL : g * NCOL + nt * P],
+                                in0=ep[:, 0 : nt * P],
+                                scalar1=bias_t[:, 4 + c : 5 + c],
+                            )
+                        else:
+                            nc.scalar.activation(
+                                out=emb_t[:, c, g * NCOL : g * NCOL + nt * P],
+                                in_=ep[:, 0 : nt * P],
+                                func=ACT.Identity,
+                                bias=bias_t[:, 4 + c : 5 + c],
+                                scale=1.0,
+                            )
                 for jj in range(nt, GROUP):
                     ea = ps1.tile([P, DO], F32, name="ea", tag="ep")
                     nc.tensor.matmul_mx(
@@ -217,12 +227,15 @@ def tile_relationembedding_t_kernel(tc, sbj_vec, obj_vec, W1, b1, W2, b2, label_
             steps = [(r, l) for r in range(len(ranges)) for l in range(L)]
             m_tiles = {}
 
-            def pass1(s):
+            def pass1(s, c0, c1):
+                if s >= len(steps):
+                    return
                 r, l = steps[s]
                 j0, nb, owners = ranges[r]
-                m = mp.tile([P, NC, wmax], F32, name="m")
-                m_tiles[s] = m
-                for c in range(NC):
+                if c0 == 0:
+                    m_tiles[s] = mp.tile([P, NC, wmax], F32, name="m")
+                m = m_tiles[s]
+                for c in range(c0, c1):
                     nc.vector.tensor_scalar(
                         out=m[:, c, 0 : nb * P],
                         in0=emb_t[:, c, j0 * P : (j0 + nb) * P],
@@ -247,11 +260,11 @@ def tile_relationembedding_t_kernel(tc, sbj_vec, obj_vec, W1, b1, W2, b2, label_
                         stop=True,
                     )
 
-            def units(s):
+            def units(s, b0, b1):
                 r, l = steps[s]
                 j0, nb, owners = ranges[r]
                 m = m_tiles[s]
-                for bi in range(nb):
+                for bi in range(b0, b1):
                     if HBK > 0:
                         if BURST_EVERY > 0 and n_units[0] % BURST_EVERY == 0:
                             heartbeat(WARM_N if n_units[0] == 0 else BURST_N)
@@ -340,18 +353,19 @@ def tile_relationembedding_t_kernel(tc, sbj_vec, obj_vec, W1, b1, W2, b2, label_
 
             done = 0
             later = {}
-            for s in range(min(AHEAD, len(steps))):
-                pass1(s)
+            for s in range(AHEAD):
+                pass1(s, 0, NC)
             for s in range(len(steps)):
-                if s + AHEAD < len(steps):
-                    pass1(s + AHEAD)
-                units(s)
-                upto = (len(pieces) * (s + 1)) // len(steps)
-                while done < upto:
-                    fn, args = pieces[done]
-                    fn(*args)
-                    done += 1
                 r, l = steps[s]
+                nb = ranges[r][1]
+                for k in range(PARTS):
+                    pass1(s + AHEAD, (NC * k) // PARTS, (NC * (k + 1)) // PARTS)
+                    units(s, (nb * k) // PARTS, (nb * (k + 1)) // PARTS)
+                    upto = (len(pieces) * (s * PARTS + k + 1)) // (len(steps) * PARTS)
+                    while done < upto:
+                        fn, args = pieces[done]
+                        fn(*args)
+                        done += 1
                 if l == L - 1:
                     j0, nb, owners = ranges[r]
                     later[s + 1] = [(from_stats, (j0 + bi,)) for bi in range(nb) if owners[bi]]

@@ -18,17 +18,17 @@ NC = DO // P
 GROUP = 4
 NCOL = GROUP * P
 
-NA = 2
-NV = 6
+NA = 0
+NV = 8
 NT = NJ - NA
 AHEAD = 2
 MBUFS = 3
 PIN = True
-RB = 10
+RB = 8
 LBN = 4
 PARTS = 2
-HBK = 4
-BURST_EVERY = 128
+HBK = 5
+BURST_EVERY = 125
 BURST_N = 5
 WARM_N = 8
 NBANK = 7
@@ -64,7 +64,7 @@ def tile_relationembedding_t_kernel(tc, sbj_vec, obj_vec, W1, b1, W2, b2, label_
         lab_t = keep.tile([P, NC, L], F32, name="lab_t")
         bias_t = keep.tile([P, 8], F32, name="bias_t")
         emb_t = keep.tile([P, NC, NT * P], F32, name="emb_t")
-        emb_a = keep.tile([P, max(NA, 1), DO], F32, name="emb_a")
+        emb_a = keep.tile([P, NA, DO], F32, name="emb_a") if NA > 0 else None
         sums = keep.tile([P, NJ, L], F32, name="sums")
         w2_q = keep.tile([P, DO], U32, name="w2_q", align_bytes=64)
         w2_s = keep.tile([P, DO], U8, name="w2_s", align_bytes=64)
@@ -101,8 +101,8 @@ def tile_relationembedding_t_kernel(tc, sbj_vec, obj_vec, W1, b1, W2, b2, label_
             nc.sync.dma_start(out=w2_raw[:], in_=W2.rearrange("(t p) d -> p t d", p=P))
             lab_sb = prep.tile([P, DO], BF16, name="lab_sb")
             nc.sync.dma_start(out=lab_sb[:], in_=label_vecs)
-            b2_bc = prep.tile([P, DO], BF16, name="b2_bc")
             if NA > 0:
+                b2_bc = prep.tile([P, DO], BF16, name="b2_bc")
                 nc.sync.dma_start(out=b2_bc[:], in_=b2.partition_broadcast(P))
             load_x(8, 16)
             load_x(16, 24)
@@ -209,7 +209,7 @@ def tile_relationembedding_t_kernel(tc, sbj_vec, obj_vec, W1, b1, W2, b2, label_
         out_v = out.rearrange("(p j) l -> p j l", j=NJ)
         with ExitStack() as main:
             mp = main.enter_context(tc.tile_pool(name="mp", bufs=MBUFS))
-            ap2 = main.enter_context(tc.tile_pool(name="ap2", bufs=2))
+            ap2 = main.enter_context(tc.tile_pool(name="ap2", bufs=2)) if NA > 0 else None
             junk = main.enter_context(tc.tile_pool(name="junk", bufs=4))
             fin = main.enter_context(tc.tile_pool(name="fin", bufs=2))
             stp = main.enter_context(tc.tile_pool(name="stp", bufs=1))

@@ -12,66 +12,51 @@ ALU = mybir.AluOpType
 ACT = mybir.ActivationFunctionType
 
 P = 128
+PACK = 4
 B, DH, DO, L = 4096, 256, 512, 128
-NJ = B // P
-NC = DO // P
-GROUP = 4
-NCOL = GROUP * P
+N_BLOCKS = B // P
+N_CHUNKS = DO // P
+GROUP_BLOCKS = 4
+GROUP_COLS = GROUP_BLOCKS * P
 
-NA = 0
-NV = 8
-NT = NJ - NA
+RANGE_BLOCKS = 16
+N_RANGES = N_BLOCKS // RANGE_BLOCKS
+READ_STRIDE = 4
+VECTOR_READS = tuple(range(READ_STRIDE - 1, RANGE_BLOCKS, READ_STRIDE))
+SHARED_READ = 9
+SHARED_EVERY = 4
+N_STATS = len(VECTOR_READS) + 1
 AHEAD = 2
-MBUFS = 3
-PIN = True
-RB = 8
-LBN = 4
-PARTS = 2
-HBK = 5
-BURST_EVERY = 125
-BURST_N = 5
-WARM_N = 8
-NBANK = 7
+QUARTER = RANGE_BLOCKS // N_CHUNKS
+UNIT_BANKS = 7
+IDLE_EVERY = 5
+RUN_EVERY = 500
+RUN_PASSES = 5
+FIRST_RUN_PASSES = 8
+LABEL_PARTS = ((0, 96), (96, L))
+PART_MAX = 96
+SUMS_LATE, ROOT_LATE, STORE_LATE = 1, 2, 3
 
 FLOPS = 2 * B * (2 * DH) * DO + 2 * B * DO * DO + 4 * B * L * DO
 
 
-def split_ranges():
-    n_r = -(-NT // RB)
-    res = []
-    j0 = 0
-    v_done = 0
-    for r in range(n_r):
-        nb = NT // n_r + (1 if r < NT % n_r else 0)
-        v_upto = (NV * (r + 1)) // n_r
-        nv = v_upto - v_done
-        v_done = v_upto
-        owners = [((bi + 1) * nv) // nb > (bi * nv) // nb for bi in range(nb)]
-        res.append((j0, nb, owners))
-        j0 += nb
-    return res
-
-
 def tile_relationembedding_t_kernel(tc, sbj_vec, obj_vec, W1, b1, W2, b2, label_vecs, out):
     nc = tc.nc
-    ranges = split_ranges()
-    wmax = max(nb for (j0, nb, owners) in ranges) * P
     with ExitStack() as ctx:
-        ctx.enter_context(nc.allow_non_contiguous_dma(reason="rows of 512 bytes and more"))
+        ctx.enter_context(nc.allow_non_contiguous_dma(reason="rows of 128 bytes and more"))
         keep = ctx.enter_context(tc.tile_pool(name="keep", bufs=1))
         ident_f = keep.tile([P, P], F32, name="ident_f")
         make_identity(nc, ident_f[:])
-        lab_t = keep.tile([P, NC, L], F32, name="lab_t")
+        lab_t = keep.tile([P, N_CHUNKS, L], F32, name="lab_t")
         bias_t = keep.tile([P, 8], F32, name="bias_t")
-        emb_t = keep.tile([P, NC, NT * P], F32, name="emb_t")
-        emb_a = keep.tile([P, NA, DO], F32, name="emb_a") if NA > 0 else None
-        sums = keep.tile([P, NJ, L], F32, name="sums")
+        emb_t = keep.tile([P, N_CHUNKS, B], F32, name="emb_t")
+        sums = keep.tile([P, N_BLOCKS, L], F32, name="sums")
         w2_q = keep.tile([P, DO], U32, name="w2_q", align_bytes=64)
         w2_s = keep.tile([P, DO], U8, name="w2_s", align_bytes=64)
 
-        with tc.tile_pool(name="prep", bufs=1) as prep, tc.tile_pool(name="work", bufs=2) as work, tc.psum_pool(
-            name="ps1", bufs=2
-        ) as ps1:
+        with tc.tile_pool(name="prep", bufs=1) as prep, tc.tile_pool(name="work", bufs=3) as work, tc.psum_pool(
+            name="ps_t", bufs=2
+        ) as ps_t, tc.psum_pool(name="ps_h", bufs=3) as ps_h, tc.psum_pool(name="ps_e", bufs=3) as ps_e:
             one = prep.tile([P, 1], F32, name="one")
             nc.vector.memset(one[:], 1.0)
             nc.scalar.activation(out=one[:], in_=one[:], func=ACT.Sqrt)
@@ -81,35 +66,33 @@ def tile_relationembedding_t_kernel(tc, sbj_vec, obj_vec, W1, b1, W2, b2, label_
             rows = prep.tile([P, P], BF16, name="rows")
             nc.vector.memset(rows[:], 0.0)
 
-            x_all = prep.tile([P, NJ, 2 * DH], BF16, name="x_all")
-            sbj_v = sbj_vec.rearrange("(p j) k -> p j k", j=NJ)
-            obj_v = obj_vec.rearrange("(p j) k -> p j k", j=NJ)
+            x_all = prep.tile([P, N_BLOCKS, 2 * DH], BF16, name="x_all")
+            sbj_v = sbj_vec.rearrange("(p j) k -> p j k", j=N_BLOCKS)
+            obj_v = obj_vec.rearrange("(p j) k -> p j k", j=N_BLOCKS)
 
             def load_x(j0, j1):
                 nc.sync.dma_start(out=x_all[:, j0:j1, 0:DH], in_=sbj_v[:, j0:j1, :])
                 nc.sync.dma_start(out=x_all[:, j0:j1, DH : 2 * DH], in_=obj_v[:, j0:j1, :])
 
-            w1_raw = prep.tile([P, 4, DO], BF16, name="w1_raw")
+            w1_raw = prep.tile([P, PACK, DO], BF16, name="w1_raw")
             nc.sync.dma_start(
                 out=w1_raw[:].rearrange("p (u e) h -> p u (e h)", u=2),
                 in_=W1.rearrange("(u p e) h -> p u (e h)", u=2, e=2),
             )
-            load_x(0, 8)
+            load_x(0, 4)
             nc.sync.dma_start(out=rows[0:4, :], in_=b1.rearrange("(t p) -> t p", p=P))
             nc.sync.dma_start(out=rows[4:8, :], in_=b2.rearrange("(t p) -> t p", p=P))
-            w2_raw = prep.tile([P, 4, DO], BF16, name="w2_raw")
+            w2_raw = prep.tile([P, PACK, DO], BF16, name="w2_raw")
             nc.sync.dma_start(out=w2_raw[:], in_=W2.rearrange("(t p) d -> p t d", p=P))
             lab_sb = prep.tile([P, DO], BF16, name="lab_sb")
             nc.sync.dma_start(out=lab_sb[:], in_=label_vecs)
-            if NA > 0:
-                b2_bc = prep.tile([P, DO], BF16, name="b2_bc")
-                nc.sync.dma_start(out=b2_bc[:], in_=b2.partition_broadcast(P))
+            load_x(4, 8)
             load_x(8, 16)
             load_x(16, 24)
             load_x(24, 32)
 
-            def quantise(src, codes, scales, nm):
-                grouped = work.tile([P, NCOL, 4], BF16, name=nm, tag="grouped", align_bytes=64)
+            def quantise(src, codes, scales, name):
+                grouped = work.tile([P, GROUP_COLS, PACK], BF16, name=name, tag="grouped", align_bytes=64)
                 nc.vector.tensor_copy(out=grouped[:], in_=src.rearrange("p t w -> p w t"))
                 nc.vector.quantize_mx(
                     out=codes.bitcast(FP8X4), scales=scales, in_=grouped[:].rearrange("p w t -> p (w t)")
@@ -120,21 +103,24 @@ def tile_relationembedding_t_kernel(tc, sbj_vec, obj_vec, W1, b1, W2, b2, label_
             quantise(w1_raw[:], w1_q[:], w1_s[:], "w1_g")
             quantise(w2_raw[:], w2_q[:], w2_s[:], "w2_g")
 
-            rows_t = ps1.tile([P, P], BF16, name="rows_t", tag="xt")
+            rows_t = ps_t.tile([P, P], BF16, name="rows_t", tag="xt")
             nc.tensor.transpose(rows_t[:], rows[:], ident_b[:])
             nc.vector.tensor_copy(out=bias_t[:], in_=rows_t[:, 0:8])
-            lab_ps = ps1.tile([P, NC, L], BF16, name="lab_ps", tag="xt")
-            for c in range(NC):
+            lab_ps = ps_t.tile([P, N_CHUNKS, L], BF16, name="lab_ps", tag="xt")
+            for c in range(N_CHUNKS):
                 nc.tensor.transpose(lab_ps[:, c, :], lab_sb[:, c * P : (c + 1) * P], ident_b[:])
             nc.vector.tensor_copy(out=lab_t[:], in_=lab_ps[:])
 
-            for g in range(NJ // GROUP):
-                xr = work.tile([P, GROUP, 2 * DH], BF16, name="xr")
-                nc.vector.tensor_scalar_max(out=xr[:], in0=x_all[:, g * GROUP : (g + 1) * GROUP, :], scalar1=0.0)
-                xg = work.tile([P, NCOL, 4], BF16, name="xg", align_bytes=64)
+            for g in range(N_BLOCKS // GROUP_BLOCKS):
+                cols = slice(g * GROUP_COLS, (g + 1) * GROUP_COLS)
+                xr = work.tile([P, GROUP_BLOCKS, 2 * DH], BF16, name="xr")
+                nc.vector.tensor_scalar_max(
+                    out=xr[:], in0=x_all[:, g * GROUP_BLOCKS : (g + 1) * GROUP_BLOCKS, :], scalar1=0.0
+                )
+                xg = work.tile([P, GROUP_COLS, PACK], BF16, name="xg", align_bytes=64)
                 xg_w = xg[:].rearrange("p n t -> p (n t)").bitcast(F32).rearrange("p (n u) -> p n u", u=2)
                 for half in range(2):
-                    xt = ps1.tile([P, 2, 2 * P], F32, name="xt", tag="xt")
+                    xt = ps_t.tile([P, 2, 2 * P], F32, name="xt", tag="xt")
                     for jj in range(2):
                         for u in range(2):
                             nc.tensor.transpose(
@@ -145,14 +131,14 @@ def tile_relationembedding_t_kernel(tc, sbj_vec, obj_vec, W1, b1, W2, b2, label_
                     nc.scalar.copy(
                         out=xg_w[:, half * 2 * P : (half + 1) * 2 * P, :], in_=xt[:].rearrange("p u n -> p n u")
                     )
-                x_q = work.tile([P, NCOL], U32, name="x_q", align_bytes=64)
-                x_s = work.tile([P, NCOL], U8, name="x_s", align_bytes=64)
+                x_q = work.tile([P, GROUP_COLS], U32, name="x_q", align_bytes=64)
+                x_s = work.tile([P, GROUP_COLS], U8, name="x_s", align_bytes=64)
                 nc.vector.quantize_mx(
                     out=x_q[:].bitcast(FP8X4), scales=x_s[:], in_=xg[:].rearrange("p n t -> p (n t)")
                 )
-                hb = work.tile([P, 4, NCOL], BF16, name="hb")
-                for t in range(4):
-                    hp = ps1.tile([P, NCOL], F32, name="hp")
+                hb = work.tile([P, PACK, GROUP_COLS], BF16, name="hb")
+                for t in range(PACK):
+                    hp = ps_h.tile([P, GROUP_COLS], F32, name="hp")
                     nc.tensor.matmul_mx(
                         out=hp[:],
                         lhsT=w1_q[:, t * P : (t + 1) * P].bitcast(FP8X4),
@@ -163,92 +149,72 @@ def tile_relationembedding_t_kernel(tc, sbj_vec, obj_vec, W1, b1, W2, b2, label_
                         stop=True,
                     )
                     nc.scalar.activation(out=hb[:, t, :], in_=hp[:], func=ACT.Relu, bias=bias_t[:, t : t + 1], scale=1.0)
-                h_q = work.tile([P, NCOL], U32, name="h_q", align_bytes=64)
-                h_s = work.tile([P, NCOL], U8, name="h_s", align_bytes=64)
+                h_q = work.tile([P, GROUP_COLS], U32, name="h_q", align_bytes=64)
+                h_s = work.tile([P, GROUP_COLS], U8, name="h_s", align_bytes=64)
                 quantise(hb[:], h_q[:], h_s[:], "hg")
-                nt = max(0, min(GROUP, NT - g * GROUP))
-                if nt > 0:
-                    for c in range(NC):
-                        ep = ps1.tile([P, NCOL], F32, name="ep")
-                        nc.tensor.matmul_mx(
-                            out=ep[:],
-                            lhsT=w2_q[:, c * P : (c + 1) * P].bitcast(FP8X4),
-                            lhsT_scale=w2_s[:, c * P : (c + 1) * P],
-                            rhs=h_q[:].bitcast(FP8X4),
-                            rhs_scale=h_s[:],
-                            start=True,
-                            stop=True,
-                        )
-                        if c % 2 == 0:
-                            nc.vector.tensor_scalar_add(
-                                out=emb_t[:, c, g * NCOL : g * NCOL + nt * P],
-                                in0=ep[:, 0 : nt * P],
-                                scalar1=bias_t[:, 4 + c : 5 + c],
-                            )
-                        else:
-                            nc.scalar.activation(
-                                out=emb_t[:, c, g * NCOL : g * NCOL + nt * P],
-                                in_=ep[:, 0 : nt * P],
-                                func=ACT.Identity,
-                                bias=bias_t[:, 4 + c : 5 + c],
-                                scale=1.0,
-                            )
-                for jj in range(nt, GROUP):
-                    ea = ps1.tile([P, DO], F32, name="ea", tag="ep")
+                for c in range(N_CHUNKS):
+                    ep = ps_e.tile([P, GROUP_COLS], F32, name="ep")
                     nc.tensor.matmul_mx(
-                        out=ea[:],
-                        lhsT=h_q[:, jj * P : (jj + 1) * P].bitcast(FP8X4),
-                        lhsT_scale=h_s[:, jj * P : (jj + 1) * P],
-                        rhs=w2_q[:].bitcast(FP8X4),
-                        rhs_scale=w2_s[:],
+                        out=ep[:],
+                        lhsT=w2_q[:, c * P : (c + 1) * P].bitcast(FP8X4),
+                        lhsT_scale=w2_s[:, c * P : (c + 1) * P],
+                        rhs=h_q[:].bitcast(FP8X4),
+                        rhs_scale=h_s[:],
                         start=True,
                         stop=True,
                     )
-                    nc.vector.tensor_tensor(out=emb_a[:, g * GROUP + jj - NT, :], in0=ea[:], in1=b2_bc[:], op=ALU.add)
+                    if c % 2 == 0:
+                        nc.vector.tensor_scalar_add(
+                            out=emb_t[:, c, cols], in0=ep[:, 0:GROUP_COLS], scalar1=bias_t[:, 4 + c : 5 + c]
+                        )
+                    else:
+                        nc.scalar.activation(
+                            out=emb_t[:, c, cols],
+                            in_=ep[:, 0:GROUP_COLS],
+                            func=ACT.Identity,
+                            bias=bias_t[:, 4 + c : 5 + c],
+                            scale=1.0,
+                        )
 
-        out_v = out.rearrange("(p j) l -> p j l", j=NJ)
+        out_v = out.rearrange("(p j) l -> p j l", j=N_BLOCKS)
         with ExitStack() as main:
-            mp = main.enter_context(tc.tile_pool(name="mp", bufs=MBUFS))
-            ap2 = main.enter_context(tc.tile_pool(name="ap2", bufs=2)) if NA > 0 else None
+            mp = main.enter_context(tc.tile_pool(name="mp", bufs=AHEAD + 1))
             junk = main.enter_context(tc.tile_pool(name="junk", bufs=4))
-            fin = main.enter_context(tc.tile_pool(name="fin", bufs=2))
+            fin = main.enter_context(tc.tile_pool(name="fin", bufs=1))
             stp = main.enter_context(tc.tile_pool(name="stp", bufs=1))
-            banks = main.enter_context(tc.psum_pool(name="banks", bufs=NBANK))
+            banks = main.enter_context(tc.psum_pool(name="banks", bufs=UNIT_BANKS))
             beat = main.enter_context(tc.psum_pool(name="beat", bufs=1))
-            if PIN:
-                main.enter_context(tc.manual_schedule())
+            main.enter_context(tc.manual_schedule())
 
-            stats = {}
-            for (j0, nb, owners) in ranges:
-                for bi in range(nb):
-                    if owners[bi]:
-                        stats[j0 + bi] = stp.tile([P, L, 6], F32, name="st%d" % (j0 + bi))
+            stats = []
+            shared = []
+            for r in range(N_RANGES):
+                stats.append(stp.tile([P, N_STATS, L, 6], F32, name="st%d" % r))
+                shared.append(stp.tile([P, L], F32, name="sh%d" % r))
+                nc.vector.memset(stats[r][:, N_STATS - 1, :, :], 0.0)
+                nc.vector.memset(shared[r][:], 0.0)
 
-            steps = [(r, l) for r in range(len(ranges)) for l in range(L)]
-            m_tiles = {}
+            steps = [(r, l) for r in range(N_RANGES) for l in range(L)]
+            clamped = {}
 
-            def pass1(s, c0, c1):
+            def clamp(s, c):
                 if s >= len(steps):
                     return
                 r, l = steps[s]
-                j0, nb, owners = ranges[r]
-                if c0 == 0:
-                    m_tiles[s] = mp.tile([P, NC, wmax], F32, name="m")
-                m = m_tiles[s]
-                for c in range(c0, c1):
-                    nc.vector.tensor_scalar(
-                        out=m[:, c, 0 : nb * P],
-                        in0=emb_t[:, c, j0 * P : (j0 + nb) * P],
-                        scalar1=lab_t[:, c, l : l + 1],
-                        scalar2=0.0,
-                        op0=ALU.subtract,
-                        op1=ALU.min,
-                    )
+                if c == 0:
+                    clamped[s] = mp.tile([P, N_CHUNKS, RANGE_BLOCKS * P], F32, name="m")
+                nc.vector.tensor_scalar(
+                    out=clamped[s][:, c, :],
+                    in0=emb_t[:, c, r * RANGE_BLOCKS * P : (r + 1) * RANGE_BLOCKS * P],
+                    scalar1=lab_t[:, c, l : l + 1],
+                    scalar2=0.0,
+                    op0=ALU.subtract,
+                    op1=ALU.min,
+                )
 
-            beat_ps = beat.tile([P, DO], F32, name="beat_ps") if HBK > 0 else None
-            n_units = [0]
+            beat_ps = beat.tile([P, DO], F32, name="beat_ps")
 
-            def heartbeat(n):
+            def idle_passes(n):
                 for i in range(n):
                     nc.tensor.matmul_mx(
                         out=beat_ps[:],
@@ -262,120 +228,87 @@ def tile_relationembedding_t_kernel(tc, sbj_vec, obj_vec, W1, b1, W2, b2, label_
 
             def units(s, b0, b1):
                 r, l = steps[s]
-                j0, nb, owners = ranges[r]
-                m = m_tiles[s]
                 for bi in range(b0, b1):
-                    if HBK > 0:
-                        if BURST_EVERY > 0 and n_units[0] % BURST_EVERY == 0:
-                            heartbeat(WARM_N if n_units[0] == 0 else BURST_N)
-                        elif n_units[0] % HBK == 0:
-                            heartbeat(1)
-                        n_units[0] += 1
+                    n = s * RANGE_BLOCKS + bi
+                    if n % RUN_EVERY == 0:
+                        idle_passes(FIRST_RUN_PASSES if n == 0 else RUN_PASSES)
+                    elif n % IDLE_EVERY == 0:
+                        idle_passes(1)
                     bank = banks.tile([P, DO], F32, name="bank")
-                    for c in range(NC):
-                        nc.tensor.transpose(bank[:, c * P : (c + 1) * P], m[:, c, bi * P : (bi + 1) * P], ident_f[:])
-                    if owners[bi]:
-                        nc.vector.bn_stats(out=stats[j0 + bi][:, l, :], in_=bank[:])
-                    else:
-                        js = junk.tile([P, DO], F32, name="js")
-                        nc.scalar.activation(
-                            out=js[:], in_=bank[:], func=ACT.Square, accum_out=sums[:, j0 + bi, l : l + 1]
+                    for c in range(N_CHUNKS):
+                        nc.tensor.transpose(
+                            bank[:, c * P : (c + 1) * P], clamped[s][:, c, bi * P : (bi + 1) * P], ident_f[:]
                         )
+                    if bi in VECTOR_READS:
+                        nc.vector.bn_stats(out=stats[r][:, VECTOR_READS.index(bi), l, :], in_=bank[:])
+                    elif bi == SHARED_READ and l % SHARED_EVERY == SHARED_EVERY - 1:
+                        nc.vector.bn_stats(out=stats[r][:, N_STATS - 1, l, :], in_=bank[:])
+                    else:
+                        if bi == SHARED_READ:
+                            total = shared[r][:, l : l + 1]
+                        else:
+                            total = sums[:, r * RANGE_BLOCKS + bi, l : l + 1]
+                        js = junk.tile([P, DO], F32, name="js")
+                        nc.scalar.activation(out=js[:], in_=bank[:], func=ACT.Square, accum_out=total)
 
-            roots = {}
-
-            def finish_root(j0, j1):
-                nb = j1 - j0
-                root = fin.tile([P, RB, L], F32, name="root")
-                roots[j0] = root
-                nc.scalar.activation(out=root[:, 0:nb, :], in_=sums[:, j0:j1, :], func=ACT.Sqrt)
-
-            def finish_store(j0, j1):
-                nb = j1 - j0
-                neg = fin.tile([P, RB, L], F32, name="neg")
-                nc.vector.tensor_scalar_mul(out=neg[:, 0:nb, :], in0=roots[j0][:, 0:nb, :], scalar1=-1.0)
-                nc.sync.dma_start(out=out_v[:, j0:j1, :], in_=neg[:, 0:nb, :])
-
-            def from_stats(j):
-                sv = stats[j][:].rearrange("p l (h k) -> p l h k", k=3)
-                sq = fin.tile([P, L, 2], F32, name="sq")
-                nc.vector.tensor_tensor(out=sq[:], in0=sv[:, :, :, 1], in1=sv[:, :, :, 1], op=ALU.mult)
-                tot = fin.tile([P, L, 2], F32, name="tot")
+            def sums_from_stats(r, l0, l1):
+                n = l1 - l0
+                sv = stats[r][:, :, l0:l1, :].rearrange("p v l (h k) -> p v l h k", k=3)
+                sq = fin.tile([P, N_STATS, PART_MAX, 2], F32, name="sq")
+                nc.vector.tensor_tensor(out=sq[:, :, 0:n, :], in0=sv[:, :, :, :, 1], in1=sv[:, :, :, :, 1], op=ALU.mult)
+                tot = fin.tile([P, N_STATS, PART_MAX, 2], F32, name="tot")
                 nc.vector.scalar_tensor_tensor(
-                    out=tot[:], in0=sq[:], scalar=float(DO // 2), in1=sv[:, :, :, 2], op0=ALU.mult, op1=ALU.add
+                    out=tot[:, :, 0:n, :],
+                    in0=sq[:, :, 0:n, :],
+                    scalar=float(DO // 2),
+                    in1=sv[:, :, :, :, 2],
+                    op0=ALU.mult,
+                    op1=ALU.add,
                 )
-                nc.vector.tensor_tensor(out=sums[:, j, :], in0=tot[:, :, 0], in1=tot[:, :, 1], op=ALU.add)
-
-            lb_tiles = {}
-            xs_tiles = {}
-
-            def a_load(l):
-                lb = ap2.tile([P, LBN, DO], BF16, name="lb")
-                lb_tiles[l // LBN] = lb
-                nc.sync.dma_start(
-                    out=lb[:].rearrange("p a d -> p (a d)"),
-                    in_=label_vecs[l : l + LBN, :].rearrange("a d -> (a d)").partition_broadcast(P),
+                mine_rows = sums[:, r * RANGE_BLOCKS : (r + 1) * RANGE_BLOCKS, :].rearrange(
+                    "p (v i) l -> p v i l", i=READ_STRIDE
                 )
-
-            def a_diff(l):
-                xs = ap2.tile([P, NA, DO], F32, name="xs")
-                xs_tiles[l] = xs
                 nc.vector.tensor_tensor(
-                    out=xs[:],
-                    in0=emb_a[:],
-                    in1=lb_tiles[l // LBN][:, l % LBN, :].unsqueeze(1).to_broadcast([P, NA, DO]),
-                    op=ALU.subtract,
+                    out=mine_rows[:, :, READ_STRIDE - 1, l0:l1],
+                    in0=tot[:, 0 : N_STATS - 1, 0:n, 0],
+                    in1=tot[:, 0 : N_STATS - 1, 0:n, 1],
+                    op=ALU.add,
+                )
+                part_sum = fin.tile([P, PART_MAX], F32, name="part_sum")
+                nc.vector.tensor_tensor(
+                    out=part_sum[:, 0:n], in0=tot[:, N_STATS - 1, 0:n, 0], in1=tot[:, N_STATS - 1, 0:n, 1], op=ALU.add
+                )
+                nc.vector.tensor_tensor(
+                    out=sums[:, r * RANGE_BLOCKS + SHARED_READ, l0:l1],
+                    in0=part_sum[:, 0:n],
+                    in1=shared[r][:, l0:l1],
+                    op=ALU.add,
                 )
 
-            def a_sum(l, ja):
-                jv = junk.tile([P, DO], F32, name="jv")
-                nc.vector.scalar_tensor_tensor(
-                    out=jv[:],
-                    in0=xs_tiles[l][:, ja, :],
-                    scalar=0.0,
-                    in1=xs_tiles[l][:, ja, :],
-                    op0=ALU.min,
-                    op1=ALU.mult,
-                    accum_out=sums[:, NT + ja, l : l + 1],
-                )
+            def root(r, l0, l1):
+                part = sums[:, r * RANGE_BLOCKS : (r + 1) * RANGE_BLOCKS, l0:l1]
+                nc.scalar.activation(out=part, in_=part, func=ACT.Sqrt)
 
-            pieces = []
-            if NA > 0:
-                pieces.append((a_load, (0,)))
-                pieces.append((a_diff, (0,)))
-                for l in range(L):
-                    if l % LBN == 0 and l + LBN < L:
-                        pieces.append((a_load, (l + LBN,)))
-                    if l + 1 < L:
-                        pieces.append((a_diff, (l + 1,)))
-                    for ja in range(NA):
-                        pieces.append((a_sum, (l, ja)))
+            def store(r, l0, l1):
+                part = sums[:, r * RANGE_BLOCKS : (r + 1) * RANGE_BLOCKS, l0:l1]
+                nc.vector.tensor_scalar_mul(out=part, in0=part, scalar1=-1.0)
+                nc.sync.dma_start(out=out_v[:, r * RANGE_BLOCKS : (r + 1) * RANGE_BLOCKS, l0:l1], in_=part)
 
-            done = 0
             later = {}
             for s in range(AHEAD):
-                pass1(s, 0, NC)
-            for s in range(len(steps)):
-                r, l = steps[s]
-                nb = ranges[r][1]
-                for k in range(PARTS):
-                    pass1(s + AHEAD, (NC * k) // PARTS, (NC * (k + 1)) // PARTS)
-                    units(s, (nb * k) // PARTS, (nb * (k + 1)) // PARTS)
-                    upto = (len(pieces) * (s * PARTS + k + 1)) // (len(steps) * PARTS)
-                    while done < upto:
-                        fn, args = pieces[done]
-                        fn(*args)
-                        done += 1
-                if l == L - 1:
-                    j0, nb, owners = ranges[r]
-                    later[s + 1] = [(from_stats, (j0 + bi,)) for bi in range(nb) if owners[bi]]
-                    later[s + 3] = [(finish_root, (j0, j0 + nb))]
-                    later[s + 5] = [(finish_store, (j0, j0 + nb))]
-                for fn, args in later.get(s, []):
-                    fn(*args)
-            for s in range(len(steps), len(steps) + 6):
-                for fn, args in later.get(s, []):
-                    fn(*args)
-                if s == len(steps) and NA > 0:
-                    finish_root(NT, NJ)
-                    finish_store(NT, NJ)
+                for c in range(N_CHUNKS):
+                    clamp(s, c)
+            for s in range(len(steps) + STORE_LATE + 1):
+                if s < len(steps):
+                    r, l = steps[s]
+                    for c in range(N_CHUNKS):
+                        clamp(s + AHEAD, c)
+                        units(s, c * QUARTER, (c + 1) * QUARTER)
+                    for l0, l1 in LABEL_PARTS:
+                        if l == l1 - 1:
+                            later[s + SUMS_LATE] = (sums_from_stats, r, l0, l1)
+                            later[s + ROOT_LATE] = (root, r, l0, l1)
+                            later[s + STORE_LATE] = (store, r, l0, l1)
+                if s in later:
+                    fn, r, l0, l1 = later[s]
+                    fn(r, l0, l1)

@@ -21,11 +21,16 @@ GROUP_COLS = GROUP_BLOCKS * P
 
 RANGE_BLOCKS = 16
 N_RANGES = N_BLOCKS // RANGE_BLOCKS
-READ_STRIDE = 4
-VECTOR_READS = tuple(range(READ_STRIDE - 1, RANGE_BLOCKS, READ_STRIDE))
-SHARED_READ = 9
+VECTOR_PLACES = (2, 6, 10, 12, 14)
+SHARED_PLACE = 8
 SHARED_EVERY = 4
-N_STATS = len(VECTOR_READS) + 1
+N_VECTOR = len(VECTOR_PLACES)
+N_STATS = N_VECTOR + 1
+SCALAR_PLACES = tuple(i for i in range(RANGE_BLOCKS) if i not in VECTOR_PLACES and i != SHARED_PLACE)
+PLACE_ORDER = VECTOR_PLACES + (SHARED_PLACE,) + SCALAR_PLACES
+BLOCK_AT = tuple(PLACE_ORDER.index(i) for i in range(RANGE_BLOCKS))
+VECTOR_CHUNKS = N_CHUNKS - 1
+QUARTER_COLS = RANGE_BLOCKS * P // N_CHUNKS
 AHEAD = 2
 QUARTER = RANGE_BLOCKS // N_CHUNKS
 UNIT_BANKS = 7
@@ -179,6 +184,7 @@ def tile_relationembedding_t_kernel(tc, sbj_vec, obj_vec, W1, b1, W2, b2, label_
         out_v = out.rearrange("(p j) l -> p j l", j=N_BLOCKS)
         with ExitStack() as main:
             mp = main.enter_context(tc.tile_pool(name="mp", bufs=AHEAD + 1))
+            gp = main.enter_context(tc.tile_pool(name="gp", bufs=AHEAD + 1))
             junk = main.enter_context(tc.tile_pool(name="junk", bufs=4))
             fin = main.enter_context(tc.tile_pool(name="fin", bufs=1))
             stp = main.enter_context(tc.tile_pool(name="stp", bufs=1))
@@ -196,13 +202,26 @@ def tile_relationembedding_t_kernel(tc, sbj_vec, obj_vec, W1, b1, W2, b2, label_
 
             steps = [(r, l) for r in range(N_RANGES) for l in range(L)]
             clamped = {}
+            clamped_g = {}
 
             def clamp(s, c):
                 if s >= len(steps):
                     return
                 r, l = steps[s]
+                g0 = c * QUARTER_COLS
                 if c == 0:
-                    clamped[s] = mp.tile([P, N_CHUNKS, RANGE_BLOCKS * P], F32, name="m")
+                    clamped[s] = mp.tile([P, VECTOR_CHUNKS, RANGE_BLOCKS * P], F32, name="m")
+                    clamped_g[s] = gp.tile([P, RANGE_BLOCKS * P], F32, name="mg")
+                nc.gpsimd.tensor_scalar(
+                    out=clamped_g[s][:, g0 : g0 + QUARTER_COLS],
+                    in0=emb_t[:, VECTOR_CHUNKS, r * RANGE_BLOCKS * P + g0 : r * RANGE_BLOCKS * P + g0 + QUARTER_COLS],
+                    scalar1=lab_t[:, VECTOR_CHUNKS, l : l + 1],
+                    scalar2=0.0,
+                    op0=ALU.subtract,
+                    op1=ALU.min,
+                )
+                if c == VECTOR_CHUNKS:
+                    return
                 nc.vector.tensor_scalar(
                     out=clamped[s][:, c, :],
                     in0=emb_t[:, c, r * RANGE_BLOCKS * P : (r + 1) * RANGE_BLOCKS * P],
@@ -228,23 +247,22 @@ def tile_relationembedding_t_kernel(tc, sbj_vec, obj_vec, W1, b1, W2, b2, label_
 
             def units(s, b0, b1):
                 r, l = steps[s]
-                for bi in range(b0, b1):
-                    n = s * RANGE_BLOCKS + bi
+                for place in range(b0, b1):
+                    n = s * RANGE_BLOCKS + place
+                    bi = BLOCK_AT[place]
                     if n % RUN_EVERY == 0:
                         idle_passes(FIRST_RUN_PASSES if n == 0 else RUN_PASSES)
                     elif n % IDLE_EVERY == 0:
                         idle_passes(1)
                     bank = banks.tile([P, DO], F32, name="bank")
                     for c in range(N_CHUNKS):
-                        nc.tensor.transpose(
-                            bank[:, c * P : (c + 1) * P], clamped[s][:, c, bi * P : (bi + 1) * P], ident_f[:]
-                        )
-                    if bi in VECTOR_READS:
-                        nc.vector.bn_stats(out=stats[r][:, VECTOR_READS.index(bi), l, :], in_=bank[:])
-                    elif bi == SHARED_READ and l % SHARED_EVERY == SHARED_EVERY - 1:
-                        nc.vector.bn_stats(out=stats[r][:, N_STATS - 1, l, :], in_=bank[:])
+                        cols = slice(bi * P, (bi + 1) * P)
+                        piece = clamped[s][:, c, cols] if c < VECTOR_CHUNKS else clamped_g[s][:, cols]
+                        nc.tensor.transpose(bank[:, c * P : (c + 1) * P], piece, ident_f[:])
+                    if bi < N_VECTOR or (bi == N_VECTOR and l % SHARED_EVERY == SHARED_EVERY - 1):
+                        nc.vector.bn_stats(out=stats[r][:, bi, l, :], in_=bank[:])
                     else:
-                        if bi == SHARED_READ:
+                        if bi == N_VECTOR:
                             total = shared[r][:, l : l + 1]
                         else:
                             total = sums[:, r * RANGE_BLOCKS + bi, l : l + 1]
@@ -265,13 +283,10 @@ def tile_relationembedding_t_kernel(tc, sbj_vec, obj_vec, W1, b1, W2, b2, label_
                     op0=ALU.mult,
                     op1=ALU.add,
                 )
-                mine_rows = sums[:, r * RANGE_BLOCKS : (r + 1) * RANGE_BLOCKS, :].rearrange(
-                    "p (v i) l -> p v i l", i=READ_STRIDE
-                )
                 nc.vector.tensor_tensor(
-                    out=mine_rows[:, :, READ_STRIDE - 1, l0:l1],
-                    in0=tot[:, 0 : N_STATS - 1, 0:n, 0],
-                    in1=tot[:, 0 : N_STATS - 1, 0:n, 1],
+                    out=sums[:, r * RANGE_BLOCKS : r * RANGE_BLOCKS + N_VECTOR, l0:l1],
+                    in0=tot[:, 0:N_VECTOR, 0:n, 0],
+                    in1=tot[:, 0:N_VECTOR, 0:n, 1],
                     op=ALU.add,
                 )
                 part_sum = fin.tile([P, PART_MAX], F32, name="part_sum")
@@ -279,7 +294,7 @@ def tile_relationembedding_t_kernel(tc, sbj_vec, obj_vec, W1, b1, W2, b2, label_
                     out=part_sum[:, 0:n], in0=tot[:, N_STATS - 1, 0:n, 0], in1=tot[:, N_STATS - 1, 0:n, 1], op=ALU.add
                 )
                 nc.vector.tensor_tensor(
-                    out=sums[:, r * RANGE_BLOCKS + SHARED_READ, l0:l1],
+                    out=sums[:, r * RANGE_BLOCKS + N_VECTOR, l0:l1],
                     in0=part_sum[:, 0:n],
                     in1=shared[r][:, l0:l1],
                     op=ALU.add,

@@ -22,19 +22,18 @@ GROUP_COLS = GROUP_BLOCKS * P
 RANGE_BLOCKS = 16
 N_RANGES = N_BLOCKS // RANGE_BLOCKS
 VECTOR_PLACES = (2, 6, 10, 12, 14)
-SHARED_PLACE = 8
-SHARED_EVERY = 4
 N_VECTOR = len(VECTOR_PLACES)
-N_STATS = N_VECTOR + 1
-SCALAR_PLACES = tuple(i for i in range(RANGE_BLOCKS) if i not in VECTOR_PLACES and i != SHARED_PLACE)
-PLACE_ORDER = VECTOR_PLACES + (SHARED_PLACE,) + SCALAR_PLACES
+SCALAR_PLACES = tuple(i for i in range(RANGE_BLOCKS) if i not in VECTOR_PLACES)
+PLACE_ORDER = VECTOR_PLACES + SCALAR_PLACES
 BLOCK_AT = tuple(PLACE_ORDER.index(i) for i in range(RANGE_BLOCKS))
-VECTOR_CHUNKS = N_CHUNKS - 1
-QUARTER_COLS = RANGE_BLOCKS * P // N_CHUNKS
+LAST = N_CHUNKS - 1
+GP_BLOCKS = 12
+GP_COLS = GP_BLOCKS * P
+GP_PIECE = GP_COLS // N_CHUNKS
+LOWEST = -3.4028234663852886e38
 AHEAD = 2
 QUARTER = RANGE_BLOCKS // N_CHUNKS
 UNIT_BANKS = 7
-IDLE_EVERY = 5
 RUN_EVERY = 500
 RUN_PASSES = 5
 FIRST_RUN_PASSES = 8
@@ -53,6 +52,7 @@ def tile_relationembedding_t_kernel(tc, sbj_vec, obj_vec, W1, b1, W2, b2, label_
         ident_f = keep.tile([P, P], F32, name="ident_f")
         make_identity(nc, ident_f[:])
         lab_t = keep.tile([P, N_CHUNKS, L], F32, name="lab_t")
+        neg_t = keep.tile([P, L], F32, name="neg_t")
         bias_t = keep.tile([P, 8], F32, name="bias_t")
         emb_t = keep.tile([P, N_CHUNKS, B], F32, name="emb_t")
         sums = keep.tile([P, N_BLOCKS, L], F32, name="sums")
@@ -115,6 +115,7 @@ def tile_relationembedding_t_kernel(tc, sbj_vec, obj_vec, W1, b1, W2, b2, label_
             for c in range(N_CHUNKS):
                 nc.tensor.transpose(lab_ps[:, c, :], lab_sb[:, c * P : (c + 1) * P], ident_b[:])
             nc.vector.tensor_copy(out=lab_t[:], in_=lab_ps[:])
+            nc.vector.tensor_scalar_mul(out=neg_t[:], in0=lab_t[:, LAST, :], scalar1=-1.0)
 
             for g in range(N_BLOCKS // GROUP_BLOCKS):
                 cols = slice(g * GROUP_COLS, (g + 1) * GROUP_COLS)
@@ -193,12 +194,8 @@ def tile_relationembedding_t_kernel(tc, sbj_vec, obj_vec, W1, b1, W2, b2, label_
             main.enter_context(tc.manual_schedule())
 
             stats = []
-            shared = []
             for r in range(N_RANGES):
-                stats.append(stp.tile([P, N_STATS, L, 6], F32, name="st%d" % r))
-                shared.append(stp.tile([P, L], F32, name="sh%d" % r))
-                nc.vector.memset(stats[r][:, N_STATS - 1, :, :], 0.0)
-                nc.vector.memset(shared[r][:], 0.0)
+                stats.append(stp.tile([P, N_VECTOR, L, 6], F32, name="st%d" % r))
 
             steps = [(r, l) for r in range(N_RANGES) for l in range(L)]
             clamped = {}
@@ -208,23 +205,24 @@ def tile_relationembedding_t_kernel(tc, sbj_vec, obj_vec, W1, b1, W2, b2, label_
                 if s >= len(steps):
                     return
                 r, l = steps[s]
-                g0 = c * QUARTER_COLS
+                first = r * RANGE_BLOCKS * P
                 if c == 0:
-                    clamped[s] = mp.tile([P, VECTOR_CHUNKS, RANGE_BLOCKS * P], F32, name="m")
-                    clamped_g[s] = gp.tile([P, RANGE_BLOCKS * P], F32, name="mg")
+                    clamped[s] = mp.tile([P, N_CHUNKS * RANGE_BLOCKS * P - GP_COLS], F32, name="m")
+                    clamped_g[s] = gp.tile([P, GP_COLS], F32, name="mg")
+                g0 = c * GP_PIECE
                 nc.gpsimd.tensor_scalar(
-                    out=clamped_g[s][:, g0 : g0 + QUARTER_COLS],
-                    in0=emb_t[:, VECTOR_CHUNKS, r * RANGE_BLOCKS * P + g0 : r * RANGE_BLOCKS * P + g0 + QUARTER_COLS],
-                    scalar1=lab_t[:, VECTOR_CHUNKS, l : l + 1],
-                    scalar2=0.0,
-                    op0=ALU.subtract,
-                    op1=ALU.min,
+                    out=clamped_g[s][:, g0 : g0 + GP_PIECE],
+                    in0=emb_t[:, LAST, first + g0 : first + g0 + GP_PIECE],
+                    scalar1=lab_t[:, LAST, l : l + 1],
+                    scalar2=LOWEST,
+                    op0=ALU.min,
+                    op1=ALU.max,
                 )
-                if c == VECTOR_CHUNKS:
-                    return
+                skip = GP_COLS if c == LAST else 0
+                m0 = c * RANGE_BLOCKS * P
                 nc.vector.tensor_scalar(
-                    out=clamped[s][:, c, :],
-                    in0=emb_t[:, c, r * RANGE_BLOCKS * P : (r + 1) * RANGE_BLOCKS * P],
+                    out=clamped[s][:, m0 : m0 + RANGE_BLOCKS * P - skip],
+                    in0=emb_t[:, c, first + skip : first + RANGE_BLOCKS * P],
                     scalar1=lab_t[:, c, l : l + 1],
                     scalar2=0.0,
                     op0=ALU.subtract,
@@ -252,29 +250,43 @@ def tile_relationembedding_t_kernel(tc, sbj_vec, obj_vec, W1, b1, W2, b2, label_
                     bi = BLOCK_AT[place]
                     if n % RUN_EVERY == 0:
                         idle_passes(FIRST_RUN_PASSES if n == 0 else RUN_PASSES)
-                    elif n % IDLE_EVERY == 0:
-                        idle_passes(1)
                     bank = banks.tile([P, DO], F32, name="bank")
                     for c in range(N_CHUNKS):
-                        cols = slice(bi * P, (bi + 1) * P)
-                        piece = clamped[s][:, c, cols] if c < VECTOR_CHUNKS else clamped_g[s][:, cols]
-                        nc.tensor.transpose(bank[:, c * P : (c + 1) * P], piece, ident_f[:])
-                    if bi < N_VECTOR or (bi == N_VECTOR and l % SHARED_EVERY == SHARED_EVERY - 1):
+                        part = bank[:, c * P : (c + 1) * P]
+                        b0c = bi * P
+                        if c == LAST and bi < GP_BLOCKS:
+                            nc.tensor.matmul(
+                                part,
+                                lhsT=clamped_g[s][:, b0c : b0c + P],
+                                rhs=ident_f[:],
+                                start=True,
+                                stop=False,
+                                is_transpose=True,
+                            )
+                            nc.tensor.matmul(
+                                part,
+                                lhsT=neg_t[:, l : l + 1].to_broadcast([P, P]),
+                                rhs=ident_f[:],
+                                start=False,
+                                stop=True,
+                                is_transpose=True,
+                            )
+                        else:
+                            m0 = c * RANGE_BLOCKS * P + b0c - (GP_COLS if c == LAST else 0)
+                            nc.tensor.transpose(part, clamped[s][:, m0 : m0 + P], ident_f[:])
+                    if bi < N_VECTOR:
                         nc.vector.bn_stats(out=stats[r][:, bi, l, :], in_=bank[:])
                     else:
-                        if bi == N_VECTOR:
-                            total = shared[r][:, l : l + 1]
-                        else:
-                            total = sums[:, r * RANGE_BLOCKS + bi, l : l + 1]
+                        total = sums[:, r * RANGE_BLOCKS + bi, l : l + 1]
                         js = junk.tile([P, DO], F32, name="js")
                         nc.scalar.activation(out=js[:], in_=bank[:], func=ACT.Square, accum_out=total)
 
             def sums_from_stats(r, l0, l1):
                 n = l1 - l0
                 sv = stats[r][:, :, l0:l1, :].rearrange("p v l (h k) -> p v l h k", k=3)
-                sq = fin.tile([P, N_STATS, PART_MAX, 2], F32, name="sq")
+                sq = fin.tile([P, N_VECTOR, PART_MAX, 2], F32, name="sq")
                 nc.vector.tensor_tensor(out=sq[:, :, 0:n, :], in0=sv[:, :, :, :, 1], in1=sv[:, :, :, :, 1], op=ALU.mult)
-                tot = fin.tile([P, N_STATS, PART_MAX, 2], F32, name="tot")
+                tot = fin.tile([P, N_VECTOR, PART_MAX, 2], F32, name="tot")
                 nc.vector.scalar_tensor_tensor(
                     out=tot[:, :, 0:n, :],
                     in0=sq[:, :, 0:n, :],
@@ -287,16 +299,6 @@ def tile_relationembedding_t_kernel(tc, sbj_vec, obj_vec, W1, b1, W2, b2, label_
                     out=sums[:, r * RANGE_BLOCKS : r * RANGE_BLOCKS + N_VECTOR, l0:l1],
                     in0=tot[:, 0:N_VECTOR, 0:n, 0],
                     in1=tot[:, 0:N_VECTOR, 0:n, 1],
-                    op=ALU.add,
-                )
-                part_sum = fin.tile([P, PART_MAX], F32, name="part_sum")
-                nc.vector.tensor_tensor(
-                    out=part_sum[:, 0:n], in0=tot[:, N_STATS - 1, 0:n, 0], in1=tot[:, N_STATS - 1, 0:n, 1], op=ALU.add
-                )
-                nc.vector.tensor_tensor(
-                    out=sums[:, r * RANGE_BLOCKS + N_VECTOR, l0:l1],
-                    in0=part_sum[:, 0:n],
-                    in1=shared[r][:, l0:l1],
                     op=ALU.add,
                 )
 

@@ -21,7 +21,7 @@ GROUP_COLS = GROUP_BLOCKS * P
 
 RANGE_BLOCKS = 16
 N_RANGES = N_BLOCKS // RANGE_BLOCKS
-VECTOR_PLACES = (2, 6, 10, 12, 14)
+VECTOR_PLACES = (3, 5, 9, 11, 13)
 N_VECTOR = len(VECTOR_PLACES)
 SCALAR_PLACES = tuple(i for i in range(RANGE_BLOCKS) if i not in VECTOR_PLACES)
 PLACE_ORDER = VECTOR_PLACES + SCALAR_PLACES
@@ -29,10 +29,13 @@ BLOCK_AT = tuple(PLACE_ORDER.index(i) for i in range(RANGE_BLOCKS))
 LAST = N_CHUNKS - 1
 GP_BLOCKS = 12
 GP_COLS = GP_BLOCKS * P
-GP_PIECE = GP_COLS // N_CHUNKS
+GP_FIRST = 4 * P
+RANGE_COLS = RANGE_BLOCKS * P
+SLOT = (2, 0, 3, 1)
+TOUCH = 2
 LOWEST = -3.4028234663852886e38
 AHEAD = 2
-QUARTER = RANGE_BLOCKS // N_CHUNKS
+HALF = RANGE_BLOCKS // 2
 UNIT_BANKS = 7
 RUN_EVERY = 500
 RUN_PASSES = 5
@@ -185,7 +188,6 @@ def tile_relationembedding_t_kernel(tc, sbj_vec, obj_vec, W1, b1, W2, b2, label_
         out_v = out.rearrange("(p j) l -> p j l", j=N_BLOCKS)
         with ExitStack() as main:
             mp = main.enter_context(tc.tile_pool(name="mp", bufs=AHEAD + 1))
-            gp = main.enter_context(tc.tile_pool(name="gp", bufs=AHEAD + 1))
             junk = main.enter_context(tc.tile_pool(name="junk", bufs=4))
             fin = main.enter_context(tc.tile_pool(name="fin", bufs=1))
             stp = main.enter_context(tc.tile_pool(name="stp", bufs=1))
@@ -199,35 +201,44 @@ def tile_relationembedding_t_kernel(tc, sbj_vec, obj_vec, W1, b1, W2, b2, label_
 
             steps = [(r, l) for r in range(N_RANGES) for l in range(L)]
             clamped = {}
-            clamped_g = {}
+            emb_flat = emb_t[:].rearrange("p c b -> p (c b)")
 
-            def clamp(s, c):
-                if s >= len(steps):
-                    return
+            def vector_clamp(s, c, b0, b1):
                 r, l = steps[s]
-                first = r * RANGE_BLOCKS * P
-                if c == 0:
-                    clamped[s] = mp.tile([P, N_CHUNKS * RANGE_BLOCKS * P - GP_COLS], F32, name="m")
-                    clamped_g[s] = gp.tile([P, GP_COLS], F32, name="mg")
-                g0 = c * GP_PIECE
-                nc.gpsimd.tensor_scalar(
-                    out=clamped_g[s][:, g0 : g0 + GP_PIECE],
-                    in0=emb_t[:, LAST, first + g0 : first + g0 + GP_PIECE],
-                    scalar1=lab_t[:, LAST, l : l + 1],
-                    scalar2=LOWEST,
-                    op0=ALU.min,
-                    op1=ALU.max,
-                )
-                skip = GP_COLS if c == LAST else 0
-                m0 = c * RANGE_BLOCKS * P
+                first = c * B + r * RANGE_COLS
                 nc.vector.tensor_scalar(
-                    out=clamped[s][:, m0 : m0 + RANGE_BLOCKS * P - skip],
-                    in0=emb_t[:, c, first + skip : first + RANGE_BLOCKS * P],
+                    out=clamped[s][:, SLOT[c] * RANGE_COLS + b0 : SLOT[c] * RANGE_COLS + b1],
+                    in0=emb_flat[:, first + b0 : first + b1],
                     scalar1=lab_t[:, c, l : l + 1],
                     scalar2=0.0,
                     op0=ALU.subtract,
                     op1=ALU.min,
                 )
+
+            def gpsimd_clamp(s, b0, b1):
+                r, l = steps[s]
+                first = r * RANGE_COLS
+                nc.gpsimd.tensor_scalar(
+                    out=clamped[s][:, SLOT[LAST] * RANGE_COLS + b0 : SLOT[LAST] * RANGE_COLS + b1],
+                    in0=emb_t[:, LAST, first + b0 : first + b1],
+                    scalar1=lab_t[:, LAST, l : l + 1],
+                    scalar2=LOWEST,
+                    op0=ALU.min,
+                    op1=ALU.max,
+                )
+
+            def clamp(s, half):
+                if s >= len(steps):
+                    return
+                if half == 0:
+                    clamped[s] = mp.tile([P, N_CHUNKS * RANGE_COLS], F32, name="m")
+                    vector_clamp(s, 0, 0, RANGE_COLS)
+                    vector_clamp(s, 1, 0, RANGE_COLS + TOUCH)
+                    gpsimd_clamp(s, 0, GP_FIRST)
+                else:
+                    vector_clamp(s, 2, 0, RANGE_COLS)
+                    vector_clamp(s, LAST, GP_COLS - TOUCH, RANGE_COLS)
+                    gpsimd_clamp(s, GP_FIRST, GP_COLS)
 
             beat_ps = beat.tile([P, DO], F32, name="beat_ps")
 
@@ -253,15 +264,11 @@ def tile_relationembedding_t_kernel(tc, sbj_vec, obj_vec, W1, b1, W2, b2, label_
                     bank = banks.tile([P, DO], F32, name="bank")
                     for c in range(N_CHUNKS):
                         part = bank[:, c * P : (c + 1) * P]
-                        b0c = bi * P
+                        m0 = SLOT[c] * RANGE_COLS + bi * P
+                        piece = clamped[s][:, m0 : m0 + P]
                         if c == LAST and bi < GP_BLOCKS:
                             nc.tensor.matmul(
-                                part,
-                                lhsT=clamped_g[s][:, b0c : b0c + P],
-                                rhs=ident_f[:],
-                                start=True,
-                                stop=False,
-                                is_transpose=True,
+                                part, lhsT=piece, rhs=ident_f[:], start=True, stop=False, is_transpose=True
                             )
                             nc.tensor.matmul(
                                 part,
@@ -272,8 +279,7 @@ def tile_relationembedding_t_kernel(tc, sbj_vec, obj_vec, W1, b1, W2, b2, label_
                                 is_transpose=True,
                             )
                         else:
-                            m0 = c * RANGE_BLOCKS * P + b0c - (GP_COLS if c == LAST else 0)
-                            nc.tensor.transpose(part, clamped[s][:, m0 : m0 + P], ident_f[:])
+                            nc.tensor.transpose(part, piece, ident_f[:])
                     if bi < N_VECTOR:
                         nc.vector.bn_stats(out=stats[r][:, bi, l, :], in_=bank[:])
                     else:
@@ -313,14 +319,14 @@ def tile_relationembedding_t_kernel(tc, sbj_vec, obj_vec, W1, b1, W2, b2, label_
 
             later = {}
             for s in range(AHEAD):
-                for c in range(N_CHUNKS):
-                    clamp(s, c)
+                for half in range(2):
+                    clamp(s, half)
             for s in range(len(steps) + STORE_LATE + 1):
                 if s < len(steps):
                     r, l = steps[s]
-                    for c in range(N_CHUNKS):
-                        clamp(s + AHEAD, c)
-                        units(s, c * QUARTER, (c + 1) * QUARTER)
+                    for half in range(2):
+                        clamp(s + AHEAD, half)
+                        units(s, half * HALF, (half + 1) * HALF)
                     for l0, l1 in LABEL_PARTS:
                         if l == l1 - 1:
                             later[s + SUMS_LATE] = (sums_from_stats, r, l0, l1)

@@ -23,6 +23,8 @@ RANGE_BLOCKS = 16
 N_RANGES = N_BLOCKS // RANGE_BLOCKS
 VECTOR_PLACES = (3, 5, 9, 11, 13)
 N_VECTOR = len(VECTOR_PLACES)
+SHARED = N_VECTOR - 1
+SHARED_EVERY = 4
 SCALAR_PLACES = tuple(i for i in range(RANGE_BLOCKS) if i not in VECTOR_PLACES)
 PLACE_ORDER = VECTOR_PLACES + SCALAR_PLACES
 BLOCK_AT = tuple(PLACE_ORDER.index(i) for i in range(RANGE_BLOCKS))
@@ -32,12 +34,12 @@ GP_COLS = GP_BLOCKS * P
 GP_FIRST = 4 * P
 RANGE_COLS = RANGE_BLOCKS * P
 SLOT = (2, 0, 3, 1)
-TOUCH = 2
+TOUCH = 4
 LOWEST = -3.4028234663852886e38
 AHEAD = 2
 HALF = RANGE_BLOCKS // 2
-UNIT_BANKS = 7
-RUN_EVERY = 500
+UNIT_BANKS = 8
+RUN_EVERY = 1024
 RUN_PASSES = 5
 FIRST_RUN_PASSES = 8
 LABEL_PARTS = ((0, 96), (96, L))
@@ -192,12 +194,15 @@ def tile_relationembedding_t_kernel(tc, sbj_vec, obj_vec, W1, b1, W2, b2, label_
             fin = main.enter_context(tc.tile_pool(name="fin", bufs=1))
             stp = main.enter_context(tc.tile_pool(name="stp", bufs=1))
             banks = main.enter_context(tc.psum_pool(name="banks", bufs=UNIT_BANKS))
-            beat = main.enter_context(tc.psum_pool(name="beat", bufs=1))
             main.enter_context(tc.manual_schedule())
 
             stats = []
+            shared = []
             for r in range(N_RANGES):
                 stats.append(stp.tile([P, N_VECTOR, L, 6], F32, name="st%d" % r))
+                shared.append(stp.tile([P, L], F32, name="sh%d" % r))
+                nc.vector.memset(stats[r][:, SHARED, :, :], 0.0)
+                nc.vector.memset(shared[r][:], 0.0)
 
             steps = [(r, l) for r in range(N_RANGES) for l in range(L)]
             clamped = {}
@@ -240,12 +245,11 @@ def tile_relationembedding_t_kernel(tc, sbj_vec, obj_vec, W1, b1, W2, b2, label_
                     vector_clamp(s, LAST, GP_COLS - TOUCH, RANGE_COLS)
                     gpsimd_clamp(s, GP_FIRST, GP_COLS)
 
-            beat_ps = beat.tile([P, DO], F32, name="beat_ps")
-
             def idle_passes(n):
+                bank = banks.tile([P, DO], F32, name="bank")
                 for i in range(n):
                     nc.tensor.matmul_mx(
-                        out=beat_ps[:],
+                        out=bank[:],
                         lhsT=w2_q[:, 0:P].bitcast(FP8X4),
                         lhsT_scale=w2_s[:, 0:P],
                         rhs=w2_q[:].bitcast(FP8X4),
@@ -280,10 +284,13 @@ def tile_relationembedding_t_kernel(tc, sbj_vec, obj_vec, W1, b1, W2, b2, label_
                             )
                         else:
                             nc.tensor.transpose(part, piece, ident_f[:])
-                    if bi < N_VECTOR:
+                    if bi < SHARED or (bi == SHARED and l % SHARED_EVERY != SHARED_EVERY - 1):
                         nc.vector.bn_stats(out=stats[r][:, bi, l, :], in_=bank[:])
                     else:
-                        total = sums[:, r * RANGE_BLOCKS + bi, l : l + 1]
+                        if bi == SHARED:
+                            total = shared[r][:, l : l + 1]
+                        else:
+                            total = sums[:, r * RANGE_BLOCKS + bi, l : l + 1]
                         js = junk.tile([P, DO], F32, name="js")
                         nc.scalar.activation(out=js[:], in_=bank[:], func=ACT.Square, accum_out=total)
 
@@ -307,6 +314,8 @@ def tile_relationembedding_t_kernel(tc, sbj_vec, obj_vec, W1, b1, W2, b2, label_
                     in1=tot[:, 0:N_VECTOR, 0:n, 1],
                     op=ALU.add,
                 )
+                both = sums[:, r * RANGE_BLOCKS + SHARED, l0:l1]
+                nc.vector.tensor_tensor(out=both, in0=both, in1=shared[r][:, l0:l1], op=ALU.add)
 
             def root(r, l0, l1):
                 part = sums[:, r * RANGE_BLOCKS : (r + 1) * RANGE_BLOCKS, l0:l1]

from contextlib import ExitStack

import concourse.mybir as mybir
from concourse.masks import make_identity

F32 = mybir.dt.float32
BF16 = mybir.dt.bfloat16
U32 = mybir.dt.uint32
U8 = mybir.dt.uint8
FP8X4 = mybir.dt.float8_e4m3fn_x4
ALU = mybir.AluOpType
ACT = mybir.ActivationFunctionType

P = 128
PACK = 4
B, DH, DO, L = 4096, 256, 512, 128
N_BLOCKS = B // P
N_CHUNKS = DO // P
GROUP_BLOCKS = 4
GROUP_COLS = GROUP_BLOCKS * P

RANGE_BLOCKS = 16
N_RANGES = N_BLOCKS // RANGE_BLOCKS
VECTOR_PLACES = (3, 5, 9, 11, 13)
N_VECTOR = len(VECTOR_PLACES)
SHARED = N_VECTOR - 1
SHARED_EVERY = 4
SCALAR_PLACES = tuple(i for i in range(RANGE_BLOCKS) if i not in VECTOR_PLACES)
PLACE_ORDER = VECTOR_PLACES + SCALAR_PLACES
BLOCK_AT = tuple(PLACE_ORDER.index(i) for i in range(RANGE_BLOCKS))
LAST = N_CHUNKS - 1
GP_BLOCKS = 12
GP_COLS = GP_BLOCKS * P
GP_FIRST = 4 * P
RANGE_COLS = RANGE_BLOCKS * P
SLOT = (2, 0, 3, 1)
TOUCH = 4
LOWEST = -3.4028234663852886e38
AHEAD = 2
HALF = RANGE_BLOCKS // 2
UNIT_BANKS = 8
RUN_EVERY = 1024
RUN_PASSES = 5
FIRST_RUN_PASSES = 8
LABEL_PARTS = ((0, 96), (96, L))
PART_MAX = 96
SUMS_LATE, ROOT_LATE, STORE_LATE = 1, 2, 3

FLOPS = 2 * B * (2 * DH) * DO + 2 * B * DO * DO + 4 * B * L * DO


def tile_relationembedding_t_kernel(tc, sbj_vec, obj_vec, W1, b1, W2, b2, label_vecs, out):
    nc = tc.nc
    with ExitStack() as ctx:
        ctx.enter_context(nc.allow_non_contiguous_dma(reason="rows of 128 bytes and more"))
        keep = ctx.enter_context(tc.tile_pool(name="keep", bufs=1))
        ident_f = keep.tile([P, P], F32, name="ident_f")
        make_identity(nc, ident_f[:])
        lab_t = keep.tile([P, N_CHUNKS, L], F32, name="lab_t")
        neg_t = keep.tile([P, L], F32, name="neg_t")
        bias_t = keep.tile([P, 8], F32, name="bias_t")
        emb_t = keep.tile([P, N_CHUNKS, B], F32, name="emb_t")
        sums = keep.tile([P, N_BLOCKS, L], F32, name="sums")
        w2_q = keep.tile([P, DO], U32, name="w2_q", align_bytes=64)
        w2_s = keep.tile([P, DO], U8, name="w2_s", align_bytes=64)

        with tc.tile_pool(name="prep", bufs=1) as prep, tc.tile_pool(name="work", bufs=3) as work, tc.psum_pool(
            name="ps_t", bufs=2
        ) as ps_t, tc.psum_pool(name="ps_h", bufs=3) as ps_h, tc.psum_pool(name="ps_e", bufs=3) as ps_e:
            one = prep.tile([P, 1], F32, name="one")
            nc.vector.memset(one[:], 1.0)
            nc.scalar.activation(out=one[:], in_=one[:], func=ACT.Sqrt)

            ident_b = prep.tile([P, P], BF16, name="ident_b")
            make_identity(nc, ident_b[:])
            rows = prep.tile([P, P], BF16, name="rows")
            nc.vector.memset(rows[:], 0.0)

            x_all = prep.tile([P, N_BLOCKS, 2 * DH], BF16, name="x_all")
            sbj_v = sbj_vec.rearrange("(p j) k -> p j k", j=N_BLOCKS)
            obj_v = obj_vec.rearrange("(p j) k -> p j k", j=N_BLOCKS)

            def load_x(j0, j1):
                nc.sync.dma_start(out=x_all[:, j0:j1, 0:DH], in_=sbj_v[:, j0:j1, :])
                nc.sync.dma_start(out=x_all[:, j0:j1, DH : 2 * DH], in_=obj_v[:, j0:j1, :])

            w1_raw = prep.tile([P, PACK, DO], BF16, name="w1_raw")
            nc.sync.dma_start(
                out=w1_raw[:].rearrange("p (u e) h -> p u (e h)", u=2),
                in_=W1.rearrange("(u p e) h -> p u (e h)", u=2, e=2),
            )
            load_x(0, 4)
            nc.sync.dma_start(out=rows[0:4, :], in_=b1.rearrange("(t p) -> t p", p=P))
            nc.sync.dma_start(out=rows[4:8, :], in_=b2.rearrange("(t p) -> t p", p=P))
            w2_raw = prep.tile([P, PACK, DO], BF16, name="w2_raw")
            nc.sync.dma_start(out=w2_raw[:], in_=W2.rearrange("(t p) d -> p t d", p=P))
            lab_sb = prep.tile([P, DO], BF16, name="lab_sb")
            nc.sync.dma_start(out=lab_sb[:], in_=label_vecs)
            load_x(4, 8)
            load_x(8, 16)
            load_x(16, 24)
            load_x(24, 32)

            def quantise(src, codes, scales, name):
                grouped = work.tile([P, GROUP_COLS, PACK], BF16, name=name, tag="grouped", align_bytes=64)
                nc.vector.tensor_copy(out=grouped[:], in_=src.rearrange("p t w -> p w t"))
                nc.vector.quantize_mx(
                    out=codes.bitcast(FP8X4), scales=scales, in_=grouped[:].rearrange("p w t -> p (w t)")
                )

            w1_q = prep.tile([P, DO], U32, name="w1_q", align_bytes=64)
            w1_s = prep.tile([P, DO], U8, name="w1_s", align_bytes=64)
            quantise(w1_raw[:], w1_q[:], w1_s[:], "w1_g")
            quantise(w2_raw[:], w2_q[:], w2_s[:], "w2_g")

            rows_t = ps_t.tile([P, P], BF16, name="rows_t", tag="xt")
            nc.tensor.transpose(rows_t[:], rows[:], ident_b[:])
            nc.vector.tensor_copy(out=bias_t[:], in_=rows_t[:, 0:8])
            lab_ps = ps_t.tile([P, N_CHUNKS, L], BF16, name="lab_ps", tag="xt")
            for c in range(N_CHUNKS):
                nc.tensor.transpose(lab_ps[:, c, :], lab_sb[:, c * P : (c + 1) * P], ident_b[:])
            nc.vector.tensor_copy(out=lab_t[:], in_=lab_ps[:])
            nc.vector.tensor_scalar_mul(out=neg_t[:], in0=lab_t[:, LAST, :], scalar1=-1.0)

            for g in range(N_BLOCKS // GROUP_BLOCKS):
                cols = slice(g * GROUP_COLS, (g + 1) * GROUP_COLS)
                xr = work.tile([P, GROUP_BLOCKS, 2 * DH], BF16, name="xr")
                nc.vector.tensor_scalar_max(
                    out=xr[:], in0=x_all[:, g * GROUP_BLOCKS : (g + 1) * GROUP_BLOCKS, :], scalar1=0.0
                )
                xg = work.tile([P, GROUP_COLS, PACK], BF16, name="xg", align_bytes=64)
                xg_w = xg[:].rearrange("p n t -> p (n t)").bitcast(F32).rearrange("p (n u) -> p n u", u=2)
                for half in range(2):
                    xt = ps_t.tile([P, 2, 2 * P], F32, name="xt", tag="xt")
                    for jj in range(2):
                        for u in range(2):
                            nc.tensor.transpose(
                                xt[:, u, jj * P : (jj + 1) * P],
                                xr[:, 2 * half + jj, u * DH : (u + 1) * DH].bitcast(F32),
                                ident_f[:],
                            )
                    nc.scalar.copy(
                        out=xg_w[:, half * 2 * P : (half + 1) * 2 * P, :], in_=xt[:].rearrange("p u n -> p n u")
                    )
                x_q = work.tile([P, GROUP_COLS], U32, name="x_q", align_bytes=64)
                x_s = work.tile([P, GROUP_COLS], U8, name="x_s", align_bytes=64)
                nc.vector.quantize_mx(
                    out=x_q[:].bitcast(FP8X4), scales=x_s[:], in_=xg[:].rearrange("p n t -> p (n t)")
                )
                hb = work.tile([P, PACK, GROUP_COLS], BF16, name="hb")
                for t in range(PACK):
                    hp = ps_h.tile([P, GROUP_COLS], F32, name="hp")
                    nc.tensor.matmul_mx(
                        out=hp[:],
                        lhsT=w1_q[:, t * P : (t + 1) * P].bitcast(FP8X4),
                        lhsT_scale=w1_s[:, t * P : (t + 1) * P],
                        rhs=x_q[:].bitcast(FP8X4),
                        rhs_scale=x_s[:],
                        start=True,
                        stop=True,
                    )
                    nc.scalar.activation(out=hb[:, t, :], in_=hp[:], func=ACT.Relu, bias=bias_t[:, t : t + 1], scale=1.0)
                h_q = work.tile([P, GROUP_COLS], U32, name="h_q", align_bytes=64)
                h_s = work.tile([P, GROUP_COLS], U8, name="h_s", align_bytes=64)
                quantise(hb[:], h_q[:], h_s[:], "hg")
                for c in range(N_CHUNKS):
                    ep = ps_e.tile([P, GROUP_COLS], F32, name="ep")
                    nc.tensor.matmul_mx(
                        out=ep[:],
                        lhsT=w2_q[:, c * P : (c + 1) * P].bitcast(FP8X4),
                        lhsT_scale=w2_s[:, c * P : (c + 1) * P],
                        rhs=h_q[:].bitcast(FP8X4),
                        rhs_scale=h_s[:],
                        start=True,
                        stop=True,
                    )
                    if c % 2 == 0:
                        nc.vector.tensor_scalar_add(
                            out=emb_t[:, c, cols], in0=ep[:, 0:GROUP_COLS], scalar1=bias_t[:, 4 + c : 5 + c]
                        )
                    else:
                        nc.scalar.activation(
                            out=emb_t[:, c, cols],
                            in_=ep[:, 0:GROUP_COLS],
                            func=ACT.Identity,
                            bias=bias_t[:, 4 + c : 5 + c],
                            scale=1.0,
                        )

        out_v = out.rearrange("(p j) l -> p j l", j=N_BLOCKS)
        with ExitStack() as main:
            mp = main.enter_context(tc.tile_pool(name="mp", bufs=AHEAD + 1))
            junk = main.enter_context(tc.tile_pool(name="junk", bufs=4))
            fin = main.enter_context(tc.tile_pool(name="fin", bufs=1))
            stp = main.enter_context(tc.tile_pool(name="stp", bufs=1))
            banks = main.enter_context(tc.psum_pool(name="banks", bufs=UNIT_BANKS))
            main.enter_context(tc.manual_schedule())

            stats = []
            shared = []
            for r in range(N_RANGES):
                stats.append(stp.tile([P, N_VECTOR, L, 6], F32, name="st%d" % r))
                shared.append(stp.tile([P, L], F32, name="sh%d" % r))
                nc.vector.memset(stats[r][:, SHARED, :, :], 0.0)
                nc.vector.memset(shared[r][:], 0.0)

            steps = [(r, l) for r in range(N_RANGES) for l in range(L)]
            clamped = {}
            emb_flat = emb_t[:].rearrange("p c b -> p (c b)")

            def vector_clamp(s, c, b0, b1):
                r, l = steps[s]
                first = c * B + r * RANGE_COLS
                nc.vector.tensor_scalar(
                    out=clamped[s][:, SLOT[c] * RANGE_COLS + b0 : SLOT[c] * RANGE_COLS + b1],
                    in0=emb_flat[:, first + b0 : first + b1],
                    scalar1=lab_t[:, c, l : l + 1],
                    scalar2=0.0,
                    op0=ALU.subtract,
                    op1=ALU.min,
                )

            def gpsimd_clamp(s, b0, b1):
                r, l = steps[s]
                first = r * RANGE_COLS
                nc.gpsimd.tensor_scalar(
                    out=clamped[s][:, SLOT[LAST] * RANGE_COLS + b0 : SLOT[LAST] * RANGE_COLS + b1],
                    in0=emb_t[:, LAST, first + b0 : first + b1],
                    scalar1=lab_t[:, LAST, l : l + 1],
                    scalar2=LOWEST,
                    op0=ALU.min,
                    op1=ALU.max,
                )

            def clamp(s, half):
                if s >= len(steps):
                    return
                if half == 0:
                    clamped[s] = mp.tile([P, N_CHUNKS * RANGE_COLS], F32, name="m")
                    vector_clamp(s, 0, 0, RANGE_COLS)
                    vector_clamp(s, 1, 0, RANGE_COLS + TOUCH)
                    gpsimd_clamp(s, 0, GP_FIRST)
                else:
                    vector_clamp(s, 2, 0, RANGE_COLS)
                    vector_clamp(s, LAST, GP_COLS - TOUCH, RANGE_COLS)
                    gpsimd_clamp(s, GP_FIRST, GP_COLS)

            def idle_passes(n):
                bank = banks.tile([P, DO], F32, name="bank")
                for i in range(n):
                    nc.tensor.matmul_mx(
                        out=bank[:],
                        lhsT=w2_q[:, 0:P].bitcast(FP8X4),
                        lhsT_scale=w2_s[:, 0:P],
                        rhs=w2_q[:].bitcast(FP8X4),
                        rhs_scale=w2_s[:],
                        start=True,
                        stop=True,
                    )

            def units(s, b0, b1):
                r, l = steps[s]
                for place in range(b0, b1):
                    n = s * RANGE_BLOCKS + place
                    bi = BLOCK_AT[place]
                    if n % RUN_EVERY == 0:
                        idle_passes(FIRST_RUN_PASSES if n == 0 else RUN_PASSES)
                    bank = banks.tile([P, DO], F32, name="bank")
                    for c in range(N_CHUNKS):
                        part = bank[:, c * P : (c + 1) * P]
                        m0 = SLOT[c] * RANGE_COLS + bi * P
                        piece = clamped[s][:, m0 : m0 + P]
                        if c == LAST and bi < GP_BLOCKS:
                            nc.tensor.matmul(
                                part, lhsT=piece, rhs=ident_f[:], start=True, stop=False, is_transpose=True
                            )
                            nc.tensor.matmul(
                                part,
                                lhsT=neg_t[:, l : l + 1].to_broadcast([P, P]),
                                rhs=ident_f[:],
                                start=False,
                                stop=True,
                                is_transpose=True,
                            )
                        else:
                            nc.tensor.transpose(part, piece, ident_f[:])
                    if bi < SHARED or (bi == SHARED and l % SHARED_EVERY != SHARED_EVERY - 1):
                        nc.vector.bn_stats(out=stats[r][:, bi, l, :], in_=bank[:])
                    else:
                        if bi == SHARED:
                            total = shared[r][:, l : l + 1]
                        else:
                            total = sums[:, r * RANGE_BLOCKS + bi, l : l + 1]
                        js = junk.tile([P, DO], F32, name="js")
                        nc.scalar.activation(out=js[:], in_=bank[:], func=ACT.Square, accum_out=total)

            def sums_from_stats(r, l0, l1):
                n = l1 - l0
                sv = stats[r][:, :, l0:l1, :].rearrange("p v l (h k) -> p v l h k", k=3)
                sq = fin.tile([P, N_VECTOR, PART_MAX, 2], F32, name="sq")
                nc.vector.tensor_tensor(out=sq[:, :, 0:n, :], in0=sv[:, :, :, :, 1], in1=sv[:, :, :, :, 1], op=ALU.mult)
                tot = fin.tile([P, N_VECTOR, PART_MAX, 2], F32, name="tot")
                nc.vector.scalar_tensor_tensor(
                    out=tot[:, :, 0:n, :],
                    in0=sq[:, :, 0:n, :],
                    scalar=float(DO // 2),
                    in1=sv[:, :, :, :, 2],
                    op0=ALU.mult,
                    op1=ALU.add,
                )
                nc.vector.tensor_tensor(
                    out=sums[:, r * RANGE_BLOCKS : r * RANGE_BLOCKS + N_VECTOR, l0:l1],
                    in0=tot[:, 0:N_VECTOR, 0:n, 0],
                    in1=tot[:, 0:N_VECTOR, 0:n, 1],
                    op=ALU.add,
                )
                both = sums[:, r * RANGE_BLOCKS + SHARED, l0:l1]
                nc.vector.tensor_tensor(out=both, in0=both, in1=shared[r][:, l0:l1], op=ALU.add)

            def root(r, l0, l1):
                part = sums[:, r * RANGE_BLOCKS : (r + 1) * RANGE_BLOCKS, l0:l1]
                nc.scalar.activation(out=part, in_=part, func=ACT.Sqrt)

            def store(r, l0, l1):
                part = sums[:, r * RANGE_BLOCKS : (r + 1) * RANGE_BLOCKS, l0:l1]
                nc.vector.tensor_scalar_mul(out=part, in0=part, scalar1=-1.0)
                nc.sync.dma_start(out=out_v[:, r * RANGE_BLOCKS : (r + 1) * RANGE_BLOCKS, l0:l1], in_=part)

            later = {}
            for s in range(AHEAD):
                for half in range(2):
                    clamp(s, half)
            for s in range(len(steps) + STORE_LATE + 1):
                if s < len(steps):
                    r, l = steps[s]
                    for half in range(2):
                        clamp(s + AHEAD, half)
                        units(s, half * HALF, (half + 1) * HALF)
                    for l0, l1 in LABEL_PARTS:
                        if l == l1 - 1:
                            later[s + SUMS_LATE] = (sums_from_stats, r, l0, l1)
                            later[s + ROOT_LATE] = (root, r, l0, l1)
                            later[s + STORE_LATE] = (store, r, l0, l1)
                if s in later:
                    fn, r, l0, l1 = later[s]
                    fn(r, l0, l1)
